import numpy as np
import ml_dtypes


def mxq(x, axis, fmt="e4m3"):
    dtype, down = {"e4m3": (ml_dtypes.float8_e4m3fn, 7), "e5m2": (ml_dtypes.float8_e5m2, 14)}[fmt]
    v = np.moveaxis(np.asarray(x, np.float32).astype(ml_dtypes.bfloat16).astype(np.float64), axis, -1)
    blocks = v.reshape(v.shape[:-1] + (-1, 32))
    amax = np.abs(blocks).max(-1, keepdims=True)
    byte = np.maximum(np.where(amax > 0, np.frexp(amax)[1] - 1 + 127, 0) - down, 1)
    scale = np.exp2(byte - 127.0)
    codes = (blocks / scale).astype(np.float32).astype(dtype).astype(np.float64)
    return np.moveaxis((codes * scale).reshape(v.shape), -1, axis)


WIDE = False


def mx_kscale(k):
    if not WIDE:
        return np.ones(k)
    levels = np.array([10, -10, 5, -5, 0])
    a = np.random.permutation(np.resize(levels, k // 512 * 4)).reshape(k // 512, 4)
    idx = np.arange(k)
    return np.exp2(a[idx // 512, idx % 128 // 32])


BF16 = ml_dtypes.bfloat16


def bf(x):
    return np.asarray(x, np.float32).astype(BF16)


def f64(x):
    return np.asarray(x).astype(np.float64)


E2M1 = np.array([0.0, 0.5, 1.0, 1.5, 2.0, 3.0, 4.0, 6.0, -0.0, -0.5, -1.0, -1.5, -2.0, -3.0, -4.0, -6.0])


def pack_weight(w, fmt):
    k, n = w.shape
    w = f64(bf(w)).reshape(k // 32, 32, n)
    amax = np.abs(w).max(1)
    if fmt == "e4m3":
        byte = np.frexp(amax)[1] - 1 + 127 - 7
    else:
        mant, ex = np.frexp(amax / 6.0)
        byte = np.where(mant > 0.5, ex, ex - 1) + 127
    byte = np.clip(np.where(amax > 0, byte, 1), 1, 254)
    scaled = (w * np.exp2(127.0 - byte)[:, None, :]).reshape(k, n).astype(np.float32)
    by_word = np.ascontiguousarray(scaled.reshape(k // 512, 128, 4, n).transpose(0, 1, 3, 2))
    if fmt == "e4m3":
        words = by_word.astype(ml_dtypes.float8_e4m3fn).view(np.uint8)
    else:
        c = by_word.astype(ml_dtypes.float4_e2m1fn).view(np.uint8) & 0xF
        words = c[..., 0::2] | (c[..., 1::2] << 4)
    return np.ascontiguousarray(words), np.ascontiguousarray(byte.astype(np.uint8).reshape(k // 512, 16, n))


def unpack_weight(words, scales, fmt):
    g, p, n, _ = words.shape
    if fmt == "e4m3":
        vals = np.ascontiguousarray(words).view(ml_dtypes.float8_e4m3fn).astype(np.float64)
    else:
        nib = np.empty((g, p, n, 4), np.uint8)
        nib[..., 0::2] = words & 0xF
        nib[..., 1::2] = words >> 4
        vals = E2M1[nib]
    vals = vals * np.repeat(np.exp2(scales.astype(np.float64) - 127.0), 8, axis=1)[..., None]
    return vals.transpose(0, 1, 3, 2).reshape(g * 512, n)


N, H, S, R, T = 4096, 512, 4, 128, 128


def setup_inputs():
    s = mx_kscale(H)
    encodings = bf(np.random.standard_normal((N, H)) * s)
    domain_encs = bf(np.random.standard_normal((S, H)) * s)
    stack = np.random.standard_normal((S, H, R)) / np.sqrt(H) / s[None, :, None]
    words, scales = pack_weight(stack.reshape(-1, R), "e4m3")
    return {"encodings": encodings,
            "domain_encs": domain_encs,
            "Us_words": words,
            "Us_scales": scales}


def reference(encodings, domain_encs, Us_words, Us_scales):
    diff = f64(encodings)[None, :, :] - f64(domain_encs)[:, None, :]
    proj = mxq(diff, 2, "e4m3") @ unpack_weight(Us_words, Us_scales, "e4m3").reshape(S, H, R)
    dist = np.sqrt(np.sum(proj * proj, axis=-1))
    z = -dist
    e = np.exp(z - z.max(axis=0, keepdims=True))
    return e / e.sum(axis=0, keepdims=True)

@@ -1,0 +1,154 @@
+from contextlib import ExitStack
+
+import concourse.mybir as mybir
+from concourse.masks import make_identity
+
+F32 = mybir.dt.float32
+BF16 = mybir.dt.bfloat16
+I32 = mybir.dt.int32
+U32 = mybir.dt.uint32
+U8 = mybir.dt.uint8
+FP8X4 = mybir.dt.float8_e4m3fn_x4
+ACT = mybir.ActivationFunctionType
+ALU = mybir.AluOpType
+AXIS = mybir.AxisListType
+
+P = 128
+TOKENS = 4096
+HIDDEN = 512
+SOURCES = 4
+RANK = 128
+PACK = 4
+HALVES = 2
+TILES = TOKENS // P
+LOAD_TILES = 4
+BANK_TILES = 2
+
+FLOPS = 2 * SOURCES * TOKENS * HIDDEN * RANK
+
+
+def tile_moe_pa_e_kernel(tc, encodings, domain_encs, Us_words, Us_scales, out):
+    nc = tc.nc
+    with ExitStack() as ctx:
+        keep = ctx.enter_context(tc.tile_pool(name="keep", bufs=1))
+        diff_pool = ctx.enter_context(tc.tile_pool(name="diff_pool", bufs=3))
+        mx_pool = ctx.enter_context(tc.tile_pool(name="mx_pool", bufs=6))
+        square_pool = ctx.enter_context(tc.tile_pool(name="square_pool", bufs=4))
+        turned_psum = ctx.enter_context(tc.psum_pool(name="turned_psum", bufs=3))
+        proj_psum = ctx.enter_context(tc.psum_pool(name="proj_psum", bufs=4))
+
+        enc_rows = encodings.rearrange("(p j) h -> p j h", j=TILES)
+        enc_sb = []
+
+        def load_tokens(c):
+            chunk = keep.tile([P, LOAD_TILES, HIDDEN], BF16, name="enc%d" % c)
+            nc.sync.dma_start(out=chunk[:], in_=enc_rows[:, c * LOAD_TILES : (c + 1) * LOAD_TILES, :])
+            enc_sb.append(chunk)
+
+        load_tokens(0)
+
+        dom_t = keep.tile([P, SOURCES, PACK], BF16)
+        nc.scalar.dma_start(out=dom_t[:], in_=domain_encs.rearrange("s (p t) -> p s t", t=PACK))
+
+        one = keep.tile([P, 1], F32)
+        nc.vector.memset(one[:], 1.0)
+        warm = keep.tile([P, 1], F32)
+        nc.scalar.activation(out=warm[:], in_=one[:], func=ACT.Sqrt)
+
+        ident = keep.tile([P, P], F32)
+        make_identity(nc, ident[:])
+
+        u_codes = keep.tile([P, SOURCES, RANK], U32, align_bytes=64)
+        nc.sync.dma_start(
+            out=u_codes[:].bitcast(I32),
+            in_=Us_words.rearrange("s p r t -> p s (r t)").bitcast(I32),
+        )
+        u_scales = keep.tile([P, SOURCES, RANK], U8, align_bytes=64)
+        nc.vector.memset(u_scales[:].bitcast(I32), 0)
+        scale_rows = Us_scales.rearrange("s (quad row) r -> row quad s r", row=4)
+        for row in range(4):
+            nc.sync.dma_start(out=u_scales[row:P:32, :, :].bitcast(I32), in_=scale_rows[row].bitcast(I32))
+
+        for c in range(1, TILES // LOAD_TILES):
+            load_tokens(c)
+
+        enc_t = []
+        for bank in range(TILES // BANK_TILES):
+            turned = turned_psum.tile([P, BANK_TILES, HALVES, P], F32)
+            for a in range(BANK_TILES):
+                j = bank * BANK_TILES + a
+                words = enc_sb[j // LOAD_TILES][:, j % LOAD_TILES, :].bitcast(F32)
+                for u in range(HALVES):
+                    nc.tensor.transpose(
+                        out=turned[:, a, u, :], in_=words[:, u : HIDDEN // 2 : HALVES], identity=ident[:]
+                    )
+            grouped = keep.tile([P, BANK_TILES, P, PACK], BF16, name="enc_t%d" % bank)
+            nc.scalar.copy(out=grouped[:].bitcast(F32), in_=turned[:].rearrange("p a u n -> p a n u"))
+            enc_t.append(grouped)
+
+        sumsq = keep.tile([P, SOURCES, TILES], F32)
+        diffs = {}
+
+        def subtract(j):
+            diff = diff_pool.tile([P, SOURCES, P, PACK], BF16, align_bytes=64)
+            shape = [P, SOURCES, P, PACK]
+            nc.vector.tensor_tensor(
+                out=diff[:],
+                in0=enc_t[j // BANK_TILES][:, j % BANK_TILES].unsqueeze(1).to_broadcast(shape),
+                in1=dom_t[:].unsqueeze(2).to_broadcast(shape),
+                op=ALU.subtract,
+            )
+            diffs[j] = diff
+
+        def project(j):
+            codes = mx_pool.tile([P, SOURCES, P], U32, align_bytes=64)
+            scales = mx_pool.tile([P, SOURCES, P], U8, align_bytes=64)
+            nc.vector.quantize_mx(
+                out=codes[:].rearrange("p s n -> p (s n)").bitcast(FP8X4),
+                scales=scales[:].rearrange("p s n -> p (s n)"),
+                in_=diffs[j][:].rearrange("p s n t -> p (s n t)"),
+            )
+            proj = proj_psum.tile([P, SOURCES, RANK], F32)
+            for s in range(SOURCES):
+                nc.tensor.matmul_mx(
+                    out=proj[:, s, :],
+                    lhsT=codes[:, s, :].bitcast(FP8X4),
+                    lhsT_scale=scales[:, s, :],
+                    rhs=u_codes[:, s, :].bitcast(FP8X4),
+                    rhs_scale=u_scales[:, s, :],
+                    start=True,
+                    stop=True,
+                )
+            squares = square_pool.tile([P, SOURCES, RANK], F32)
+            for s in range(SOURCES):
+                nc.scalar.activation(
+                    out=squares[:, s, :], in_=proj[:, s, :], func=ACT.Square, accum_out=sumsq[:, s, j : j + 1]
+                )
+
+        subtract(0)
+        for j in range(TILES):
+            if j + 1 < TILES:
+                subtract(j + 1)
+            project(j)
+
+        by_token = "p s j -> p j s"
+        spread = [P, SOURCES, TILES]
+        dist = keep.tile(spread, F32)
+        nc.scalar.activation(out=dist[:], in_=sumsq[:], func=ACT.Sqrt)
+        nearest = keep.tile([P, TILES], F32)
+        nc.vector.tensor_reduce(out=nearest[:], in_=dist[:].rearrange(by_token), axis=AXIS.X, op=ALU.min)
+        excess = keep.tile(spread, F32)
+        nc.vector.tensor_tensor(
+            out=excess[:], in0=dist[:], in1=nearest[:].unsqueeze(1).to_broadcast(spread), op=ALU.subtract
+        )
+        weight = keep.tile(spread, F32)
+        nc.scalar.activation(out=weight[:], in_=excess[:], func=ACT.Exp, scale=-1.0)
+        total = keep.tile([P, TILES], F32)
+        nc.vector.tensor_reduce(out=total[:], in_=weight[:].rearrange(by_token), axis=AXIS.X, op=ALU.add)
+        inverse = keep.tile([P, TILES], F32)
+        nc.vector.reciprocal(out=inverse[:], in_=total[:])
+        alphas = keep.tile(spread, F32)
+        nc.vector.tensor_tensor(
+            out=alphas[:], in0=weight[:], in1=inverse[:].unsqueeze(1).to_broadcast(spread), op=ALU.mult
+        )
+        nc.sync.dma_start(out=out.rearrange("s (p j) -> p s j", j=TILES), in_=alphas[:])

@@ -21,8 +21,7 @@ RANK = 128
 PACK = 4
 HALVES = 2
 TILES = TOKENS // P
-LOAD_TILES = 4
-BANK_TILES = 2
+AHEAD = 4
 
 FLOPS = 2 * SOURCES * TOKENS * HIDDEN * RANK
 
@@ -32,18 +31,16 @@ def tile_moe_pa_e_kernel(tc, encodings, domain_encs, Us_words, Us_scales, out):
     with ExitStack() as ctx:
         keep = ctx.enter_context(tc.tile_pool(name="keep", bufs=1))
         diff_pool = ctx.enter_context(tc.tile_pool(name="diff_pool", bufs=3))
-        mx_pool = ctx.enter_context(tc.tile_pool(name="mx_pool", bufs=6))
+        mx_pool = ctx.enter_context(tc.tile_pool(name="mx_pool", bufs=4))
         square_pool = ctx.enter_context(tc.tile_pool(name="square_pool", bufs=4))
-        turned_psum = ctx.enter_context(tc.psum_pool(name="turned_psum", bufs=3))
+        turned_psum = ctx.enter_context(tc.psum_pool(name="turned_psum", bufs=AHEAD))
         proj_psum = ctx.enter_context(tc.psum_pool(name="proj_psum", bufs=4))
 
         enc_rows = encodings.rearrange("(p j) h -> p j h", j=TILES)
-        enc_sb = []
+        enc_sb = keep.tile([P, TILES, HIDDEN], BF16)
 
-        def load_tokens(c):
-            chunk = keep.tile([P, LOAD_TILES, HIDDEN], BF16, name="enc%d" % c)
-            nc.sync.dma_start(out=chunk[:], in_=enc_rows[:, c * LOAD_TILES : (c + 1) * LOAD_TILES, :])
-            enc_sb.append(chunk)
+        def load_tokens(j):
+            nc.sync.dma_start(out=enc_sb[:, j, :], in_=enc_rows[:, j, :])
 
         load_tokens(0)
 
@@ -58,6 +55,8 @@ def tile_moe_pa_e_kernel(tc, encodings, domain_encs, Us_words, Us_scales, out):
         ident = keep.tile([P, P], F32)
         make_identity(nc, ident[:])
 
+        load_tokens(1)
+
         u_codes = keep.tile([P, SOURCES, RANK], U32, align_bytes=64)
         nc.sync.dma_start(
             out=u_codes[:].bitcast(I32),
@@ -69,32 +68,28 @@ def tile_moe_pa_e_kernel(tc, encodings, domain_encs, Us_words, Us_scales, out):
         for row in range(4):
             nc.sync.dma_start(out=u_scales[row:P:32, :, :].bitcast(I32), in_=scale_rows[row].bitcast(I32))
 
-        for c in range(1, TILES // LOAD_TILES):
-            load_tokens(c)
-
-        enc_t = []
-        for bank in range(TILES // BANK_TILES):
-            turned = turned_psum.tile([P, BANK_TILES, HALVES, P], F32)
-            for a in range(BANK_TILES):
-                j = bank * BANK_TILES + a
-                words = enc_sb[j // LOAD_TILES][:, j % LOAD_TILES, :].bitcast(F32)
-                for u in range(HALVES):
-                    nc.tensor.transpose(
-                        out=turned[:, a, u, :], in_=words[:, u : HIDDEN // 2 : HALVES], identity=ident[:]
-                    )
-            grouped = keep.tile([P, BANK_TILES, P, PACK], BF16, name="enc_t%d" % bank)
-            nc.scalar.copy(out=grouped[:].bitcast(F32), in_=turned[:].rearrange("p a u n -> p a n u"))
-            enc_t.append(grouped)
+        for j in range(2, TILES):
+            load_tokens(j)
 
         sumsq = keep.tile([P, SOURCES, TILES], F32)
+        turneds = {}
         diffs = {}
+
+        def turn(j):
+            turned = turned_psum.tile([P, P, HALVES], F32)
+            words = enc_sb[:, j, :].bitcast(F32)
+            for u in range(HALVES):
+                nc.tensor.transpose(
+                    out=turned[:, :, u], in_=words[:, u : HIDDEN // 2 : HALVES], identity=ident[:]
+                )
+            turneds[j] = turned
 
         def subtract(j):
             diff = diff_pool.tile([P, SOURCES, P, PACK], BF16, align_bytes=64)
             shape = [P, SOURCES, P, PACK]
             nc.vector.tensor_tensor(
                 out=diff[:],
-                in0=enc_t[j // BANK_TILES][:, j % BANK_TILES].unsqueeze(1).to_broadcast(shape),
+                in0=turneds[j][:].bitcast(BF16).unsqueeze(1).to_broadcast(shape),
                 in1=dom_t[:].unsqueeze(2).to_broadcast(shape),
                 op=ALU.subtract,
             )
@@ -125,10 +120,14 @@ def tile_moe_pa_e_kernel(tc, encodings, domain_encs, Us_words, Us_scales, out):
                     out=squares[:, s, :], in_=proj[:, s, :], func=ACT.Square, accum_out=sumsq[:, s, j : j + 1]
                 )
 
+        for j in range(AHEAD):
+            turn(j)
         subtract(0)
         for j in range(TILES):
             if j + 1 < TILES:
                 subtract(j + 1)
+            if j + AHEAD < TILES:
+                turn(j + AHEAD)
             project(j)
 
         by_token = "p s j -> p j s"

@@ -22,6 +22,9 @@ PACK = 4
 HALVES = 2
 TILES = TOKENS // P
 AHEAD = 4
+ROUND = 2
+GP_TOKENS = 16
+VE_TOKENS = P - GP_TOKENS
 
 FLOPS = 2 * SOURCES * TOKENS * HIDDEN * RANK
 
@@ -30,7 +33,8 @@ def tile_moe_pa_e_kernel(tc, encodings, domain_encs, Us_words, Us_scales, out):
     nc = tc.nc
     with ExitStack() as ctx:
         keep = ctx.enter_context(tc.tile_pool(name="keep", bufs=1))
-        diff_pool = ctx.enter_context(tc.tile_pool(name="diff_pool", bufs=3))
+        side_pool = ctx.enter_context(tc.tile_pool(name="side_pool", bufs=AHEAD))
+        diff_pool = ctx.enter_context(tc.tile_pool(name="diff_pool", bufs=2 * ROUND))
         mx_pool = ctx.enter_context(tc.tile_pool(name="mx_pool", bufs=4))
         square_pool = ctx.enter_context(tc.tile_pool(name="square_pool", bufs=4))
         turned_psum = ctx.enter_context(tc.psum_pool(name="turned_psum", bufs=AHEAD))
@@ -73,6 +77,7 @@ def tile_moe_pa_e_kernel(tc, encodings, domain_encs, Us_words, Us_scales, out):
 
         sumsq = keep.tile([P, SOURCES, TILES], F32)
         turneds = {}
+        sides = {}
         diffs = {}
 
         def turn(j):
@@ -83,14 +88,24 @@ def tile_moe_pa_e_kernel(tc, encodings, domain_encs, Us_words, Us_scales, out):
                     out=turned[:, :, u], in_=words[:, u : HIDDEN // 2 : HALVES], identity=ident[:]
                 )
             turneds[j] = turned
+            side = side_pool.tile([P, GP_TOKENS, PACK], BF16)
+            nc.scalar.copy(out=side[:].bitcast(F32), in_=turned[:, VE_TOKENS:, :])
+            sides[j] = side
 
         def subtract(j):
             diff = diff_pool.tile([P, SOURCES, P, PACK], BF16, align_bytes=64)
-            shape = [P, SOURCES, P, PACK]
+            ve_shape = [P, SOURCES, VE_TOKENS, PACK]
+            gp_shape = [P, SOURCES, GP_TOKENS, PACK]
+            nc.gpsimd.tensor_tensor(
+                out=diff[:, :, VE_TOKENS:, :],
+                in0=sides[j][:].unsqueeze(1).to_broadcast(gp_shape),
+                in1=dom_t[:].unsqueeze(2).to_broadcast(gp_shape),
+                op=ALU.subtract,
+            )
             nc.vector.tensor_tensor(
-                out=diff[:],
-                in0=turneds[j][:].bitcast(BF16).unsqueeze(1).to_broadcast(shape),
-                in1=dom_t[:].unsqueeze(2).to_broadcast(shape),
+                out=diff[:, :, :VE_TOKENS, :],
+                in0=turneds[j][:, :VE_TOKENS, :].bitcast(BF16).unsqueeze(1).to_broadcast(ve_shape),
+                in1=dom_t[:].unsqueeze(2).to_broadcast(ve_shape),
                 op=ALU.subtract,
             )
             diffs[j] = diff
@@ -122,13 +137,18 @@ def tile_moe_pa_e_kernel(tc, encodings, domain_encs, Us_words, Us_scales, out):
 
         for j in range(AHEAD):
             turn(j)
-        subtract(0)
-        for j in range(TILES):
-            if j + 1 < TILES:
-                subtract(j + 1)
-            if j + AHEAD < TILES:
-                turn(j + AHEAD)
-            project(j)
+        for j in range(ROUND):
+            subtract(j)
+        for first in range(0, TILES, ROUND):
+            this_round = range(first, first + ROUND)
+            for j in this_round:
+                if j + ROUND < TILES:
+                    subtract(j + ROUND)
+            for j in this_round:
+                if j + AHEAD < TILES:
+                    turn(j + AHEAD)
+            for j in this_round:
+                project(j)
 
         by_token = "p s j -> p j s"
         spread = [P, SOURCES, TILES]

@@ -23,7 +23,7 @@ HALVES = 2
 TILES = TOKENS // P
 AHEAD = 4
 ROUND = 2
-GP_TOKENS = 16
+GP_TOKENS = 24
 VE_TOKENS = P - GP_TOKENS
 
 FLOPS = 2 * SOURCES * TOKENS * HIDDEN * RANK

@@ -20,10 +20,13 @@ SOURCES = 4
 RANK = 128
 PACK = 4
 HALVES = 2
+QUADRANT = 32
+LIVE_ROWS = 4
 TILES = TOKENS // P
 AHEAD = 4
+PROJ_BANKS = 4
 ROUND = 2
-GP_TOKENS = 24
+GP_TOKENS = 20
 VE_TOKENS = P - GP_TOKENS
 
 FLOPS = 2 * SOURCES * TOKENS * HIDDEN * RANK
@@ -35,10 +38,10 @@ def tile_moe_pa_e_kernel(tc, encodings, domain_encs, Us_words, Us_scales, out):
         keep = ctx.enter_context(tc.tile_pool(name="keep", bufs=1))
         side_pool = ctx.enter_context(tc.tile_pool(name="side_pool", bufs=AHEAD))
         diff_pool = ctx.enter_context(tc.tile_pool(name="diff_pool", bufs=2 * ROUND))
-        mx_pool = ctx.enter_context(tc.tile_pool(name="mx_pool", bufs=4))
-        square_pool = ctx.enter_context(tc.tile_pool(name="square_pool", bufs=4))
+        mx_pool = ctx.enter_context(tc.tile_pool(name="mx_pool", bufs=PROJ_BANKS))
+        square_pool = ctx.enter_context(tc.tile_pool(name="square_pool", bufs=PROJ_BANKS))
         turned_psum = ctx.enter_context(tc.psum_pool(name="turned_psum", bufs=AHEAD))
-        proj_psum = ctx.enter_context(tc.psum_pool(name="proj_psum", bufs=4))
+        proj_psum = ctx.enter_context(tc.psum_pool(name="proj_psum", bufs=PROJ_BANKS))
 
         enc_rows = encodings.rearrange("(p j) h -> p j h", j=TILES)
         enc_sb = keep.tile([P, TILES, HIDDEN], BF16)
@@ -59,7 +62,8 @@ def tile_moe_pa_e_kernel(tc, encodings, domain_encs, Us_words, Us_scales, out):
         ident = keep.tile([P, P], F32)
         make_identity(nc, ident[:])
 
-        load_tokens(1)
+        for j in range(1, ROUND):
+            load_tokens(j)
 
         u_codes = keep.tile([P, SOURCES, RANK], U32, align_bytes=64)
         nc.sync.dma_start(
@@ -68,11 +72,13 @@ def tile_moe_pa_e_kernel(tc, encodings, domain_encs, Us_words, Us_scales, out):
         )
         u_scales = keep.tile([P, SOURCES, RANK], U8, align_bytes=64)
         nc.vector.memset(u_scales[:].bitcast(I32), 0)
-        scale_rows = Us_scales.rearrange("s (quad row) r -> row quad s r", row=4)
-        for row in range(4):
-            nc.sync.dma_start(out=u_scales[row:P:32, :, :].bitcast(I32), in_=scale_rows[row].bitcast(I32))
+        scale_rows = Us_scales.rearrange("s (quad row) r -> row quad s r", row=LIVE_ROWS)
+        for row in range(LIVE_ROWS):
+            nc.sync.dma_start(
+                out=u_scales[row:P:QUADRANT, :, :].bitcast(I32), in_=scale_rows[row].bitcast(I32)
+            )
 
-        for j in range(2, TILES):
+        for j in range(ROUND, TILES):
             load_tokens(j)
 
         sumsq = keep.tile([P, SOURCES, TILES], F32)

@@ -23,11 +23,13 @@ HALVES = 2
 QUADRANT = 32
 LIVE_ROWS = 4
 TILES = TOKENS // P
-AHEAD = 4
-PROJ_BANKS = 4
-ROUND = 2
-GP_TOKENS = 20
-VE_TOKENS = P - GP_TOKENS
+PAIR = 2
+PAIRS = TILES // PAIR
+PAIR_TOKENS = PAIR * P
+AHEAD = 3
+PROJ_BANKS = 5
+GP_TOKENS = 40
+VE_TOKENS = PAIR_TOKENS - GP_TOKENS
 
 FLOPS = 2 * SOURCES * TOKENS * HIDDEN * RANK
 
@@ -37,8 +39,8 @@ def tile_moe_pa_e_kernel(tc, encodings, domain_encs, Us_words, Us_scales, out):
     with ExitStack() as ctx:
         keep = ctx.enter_context(tc.tile_pool(name="keep", bufs=1))
         side_pool = ctx.enter_context(tc.tile_pool(name="side_pool", bufs=AHEAD))
-        diff_pool = ctx.enter_context(tc.tile_pool(name="diff_pool", bufs=2 * ROUND))
-        mx_pool = ctx.enter_context(tc.tile_pool(name="mx_pool", bufs=PROJ_BANKS))
+        diff_pool = ctx.enter_context(tc.tile_pool(name="diff_pool", bufs=2))
+        mx_pool = ctx.enter_context(tc.tile_pool(name="mx_pool", bufs=3))
         square_pool = ctx.enter_context(tc.tile_pool(name="square_pool", bufs=PROJ_BANKS))
         turned_psum = ctx.enter_context(tc.psum_pool(name="turned_psum", bufs=AHEAD))
         proj_psum = ctx.enter_context(tc.psum_pool(name="proj_psum", bufs=PROJ_BANKS))
@@ -62,7 +64,7 @@ def tile_moe_pa_e_kernel(tc, encodings, domain_encs, Us_words, Us_scales, out):
         ident = keep.tile([P, P], F32)
         make_identity(nc, ident[:])
 
-        for j in range(1, ROUND):
+        for j in range(1, PAIR):
             load_tokens(j)
 
         u_codes = keep.tile([P, SOURCES, RANK], U32, align_bytes=64)
@@ -78,7 +80,7 @@ def tile_moe_pa_e_kernel(tc, encodings, domain_encs, Us_words, Us_scales, out):
                 out=u_scales[row:P:QUADRANT, :, :].bitcast(I32), in_=scale_rows[row].bitcast(I32)
             )
 
-        for j in range(ROUND, TILES):
+        for j in range(PAIR, TILES):
             load_tokens(j)
 
         sumsq = keep.tile([P, SOURCES, TILES], F32)
@@ -86,75 +88,76 @@ def tile_moe_pa_e_kernel(tc, encodings, domain_encs, Us_words, Us_scales, out):
         sides = {}
         diffs = {}
 
-        def turn(j):
-            turned = turned_psum.tile([P, P, HALVES], F32)
-            words = enc_sb[:, j, :].bitcast(F32)
-            for u in range(HALVES):
-                nc.tensor.transpose(
-                    out=turned[:, :, u], in_=words[:, u : HIDDEN // 2 : HALVES], identity=ident[:]
-                )
-            turneds[j] = turned
+        def turn(k):
+            turned = turned_psum.tile([P, PAIR_TOKENS, HALVES], F32)
+            for h in range(PAIR):
+                words = enc_sb[:, PAIR * k + h, :].bitcast(F32)
+                for u in range(HALVES):
+                    nc.tensor.transpose(
+                        out=turned[:, h * P : (h + 1) * P, u],
+                        in_=words[:, u : HIDDEN // 2 : HALVES],
+                        identity=ident[:],
+                    )
+            turneds[k] = turned
             side = side_pool.tile([P, GP_TOKENS, PACK], BF16)
             nc.scalar.copy(out=side[:].bitcast(F32), in_=turned[:, VE_TOKENS:, :])
-            sides[j] = side
+            sides[k] = side
 
-        def subtract(j):
-            diff = diff_pool.tile([P, SOURCES, P, PACK], BF16, align_bytes=64)
+        def subtract(k):
+            diff = diff_pool.tile([P, SOURCES, PAIR_TOKENS, PACK], BF16, align_bytes=64)
             ve_shape = [P, SOURCES, VE_TOKENS, PACK]
             gp_shape = [P, SOURCES, GP_TOKENS, PACK]
             nc.gpsimd.tensor_tensor(
                 out=diff[:, :, VE_TOKENS:, :],
-                in0=sides[j][:].unsqueeze(1).to_broadcast(gp_shape),
+                in0=sides[k][:].unsqueeze(1).to_broadcast(gp_shape),
                 in1=dom_t[:].unsqueeze(2).to_broadcast(gp_shape),
                 op=ALU.subtract,
             )
             nc.vector.tensor_tensor(
                 out=diff[:, :, :VE_TOKENS, :],
-                in0=turneds[j][:, :VE_TOKENS, :].bitcast(BF16).unsqueeze(1).to_broadcast(ve_shape),
+                in0=turneds[k][:, :VE_TOKENS, :].bitcast(BF16).unsqueeze(1).to_broadcast(ve_shape),
                 in1=dom_t[:].unsqueeze(2).to_broadcast(ve_shape),
                 op=ALU.subtract,
             )
-            diffs[j] = diff
+            diffs[k] = diff
 
-        def project(j):
-            codes = mx_pool.tile([P, SOURCES, P], U32, align_bytes=64)
-            scales = mx_pool.tile([P, SOURCES, P], U8, align_bytes=64)
+        def project(k):
+            codes = mx_pool.tile([P, SOURCES, PAIR_TOKENS], U32, align_bytes=64)
+            scales = mx_pool.tile([P, SOURCES, PAIR_TOKENS], U8, align_bytes=64)
             nc.vector.quantize_mx(
                 out=codes[:].rearrange("p s n -> p (s n)").bitcast(FP8X4),
                 scales=scales[:].rearrange("p s n -> p (s n)"),
-                in_=diffs[j][:].rearrange("p s n t -> p (s n t)"),
+                in_=diffs[k][:].rearrange("p s n t -> p (s n t)"),
             )
-            proj = proj_psum.tile([P, SOURCES, RANK], F32)
-            for s in range(SOURCES):
-                nc.tensor.matmul_mx(
-                    out=proj[:, s, :],
-                    lhsT=codes[:, s, :].bitcast(FP8X4),
-                    lhsT_scale=scales[:, s, :],
-                    rhs=u_codes[:, s, :].bitcast(FP8X4),
-                    rhs_scale=u_scales[:, s, :],
-                    start=True,
-                    stop=True,
-                )
-            squares = square_pool.tile([P, SOURCES, RANK], F32)
-            for s in range(SOURCES):
-                nc.scalar.activation(
-                    out=squares[:, s, :], in_=proj[:, s, :], func=ACT.Square, accum_out=sumsq[:, s, j : j + 1]
-                )
+            for h in range(PAIR):
+                j = PAIR * k + h
+                tokens = slice(h * P, (h + 1) * P)
+                proj = proj_psum.tile([P, SOURCES, RANK], F32)
+                for s in range(SOURCES):
+                    nc.tensor.matmul_mx(
+                        out=proj[:, s, :],
+                        lhsT=codes[:, s, tokens].bitcast(FP8X4),
+                        lhsT_scale=scales[:, s, tokens],
+                        rhs=u_codes[:, s, :].bitcast(FP8X4),
+                        rhs_scale=u_scales[:, s, :],
+                        start=True,
+                        stop=True,
+                    )
+                squares = square_pool.tile([P, SOURCES, RANK], F32)
+                for s in range(SOURCES):
+                    nc.scalar.activation(
+                        out=squares[:, s, :], in_=proj[:, s, :], func=ACT.Square, accum_out=sumsq[:, s, j : j + 1]
+                    )
 
-        for j in range(AHEAD):
-            turn(j)
-        for j in range(ROUND):
-            subtract(j)
-        for first in range(0, TILES, ROUND):
-            this_round = range(first, first + ROUND)
-            for j in this_round:
-                if j + ROUND < TILES:
-                    subtract(j + ROUND)
-            for j in this_round:
-                if j + AHEAD < TILES:
-                    turn(j + AHEAD)
-            for j in this_round:
-                project(j)
+        for k in range(AHEAD):
+            turn(k)
+        subtract(0)
+        for k in range(PAIRS):
+            if k + 1 < PAIRS:
+                subtract(k + 1)
+            if k + AHEAD < PAIRS:
+                turn(k + AHEAD)
+            project(k)
 
         by_token = "p s j -> p j s"
         spread = [P, SOURCES, TILES]

@@ -26,10 +26,15 @@ TILES = TOKENS // P
 PAIR = 2
 PAIRS = TILES // PAIR
 PAIR_TOKENS = PAIR * P
-AHEAD = 3
-PROJ_BANKS = 5
+AHEAD = 2
+PROJ_BANKS = 4
+MADE_BANKS = 2
 GP_TOKENS = 40
-VE_TOKENS = PAIR_TOKENS - GP_TOKENS
+MADE_PAIRS = (6, 10, 14)
+MADE_TOKENS = P - SOURCES
+CHUNK = 32
+CHUNKS = P // CHUNK
+GP_TOKENS_MADE = 20
 
 FLOPS = 2 * SOURCES * TOKENS * HIDDEN * RANK
 
@@ -44,6 +49,8 @@ def tile_moe_pa_e_kernel(tc, encodings, domain_encs, Us_words, Us_scales, out):
         square_pool = ctx.enter_context(tc.tile_pool(name="square_pool", bufs=PROJ_BANKS))
         turned_psum = ctx.enter_context(tc.psum_pool(name="turned_psum", bufs=AHEAD))
         proj_psum = ctx.enter_context(tc.psum_pool(name="proj_psum", bufs=PROJ_BANKS))
+        made_psum = ctx.enter_context(tc.psum_pool(name="made_psum", bufs=MADE_BANKS))
+        made_pool = ctx.enter_context(tc.tile_pool(name="made_pool", bufs=2))
 
         enc_rows = encodings.rearrange("(p j) h -> p j h", j=TILES)
         enc_sb = keep.tile([P, TILES, HIDDEN], BF16)
@@ -80,7 +87,25 @@ def tile_moe_pa_e_kernel(tc, encodings, domain_encs, Us_words, Us_scales, out):
                 out=u_scales[row:P:QUADRANT, :, :].bitcast(I32), in_=scale_rows[row].bitcast(I32)
             )
 
+        sel = keep.tile([P, CHUNKS, SOURCES, CHUNK], BF16)
+        sel_shape = [P, CHUNKS, SOURCES, CHUNK]
+        nc.vector.tensor_tensor(
+            out=sel[:],
+            in0=ident[:].rearrange("p (c n) -> p c n", n=CHUNK).unsqueeze(2).to_broadcast(sel_shape),
+            in1=ident[:, MADE_TOKENS:].unsqueeze(1).unsqueeze(3).to_broadcast(sel_shape),
+            op=ALU.subtract,
+        )
+        augs = {}
+
+        def load_made(k):
+            aug = keep.tile([P, HIDDEN], BF16, name="aug%d" % k)
+            nc.sync.dma_start(out=aug[:MADE_TOKENS, :], in_=enc_rows[:MADE_TOKENS, PAIR * k, :])
+            nc.sync.dma_start(out=aug[MADE_TOKENS:, :], in_=domain_encs)
+            augs[k] = aug
+
         for j in range(PAIR, TILES):
+            if j % PAIR == 0 and (j // PAIR + 2) in MADE_PAIRS:
+                load_made(j // PAIR + 2)
             load_tokens(j)
 
         sumsq = keep.tile([P, SOURCES, TILES], F32)
@@ -99,27 +124,52 @@ def tile_moe_pa_e_kernel(tc, encodings, domain_encs, Us_words, Us_scales, out):
                         identity=ident[:],
                     )
             turneds[k] = turned
-            side = side_pool.tile([P, GP_TOKENS, PACK], BF16)
-            nc.scalar.copy(out=side[:].bitcast(F32), in_=turned[:, VE_TOKENS:, :])
+            gp_tokens = GP_TOKENS_MADE if k in MADE_PAIRS else GP_TOKENS
+            side = side_pool.tile([P, gp_tokens, PACK], BF16)
+            nc.scalar.copy(out=side[:].bitcast(F32), in_=turned[:, PAIR_TOKENS - gp_tokens :, :])
             sides[k] = side
 
+        def make(k, c):
+            if c == 0:
+                diffs[k] = made_pool.tile([P, SOURCES, PAIR_TOKENS, PACK], BF16, align_bytes=64, name="made_diff")
+            made = made_psum.tile([P, PACK, SOURCES, CHUNK], F32)
+            for t in range(PACK):
+                nc.tensor.matmul(
+                    out=made[:, t, :, :].rearrange("p s n -> p (s n)"),
+                    lhsT=augs[k][:, t:HIDDEN:PACK],
+                    rhs=sel[:, c, :, :].rearrange("p s n -> p (s n)"),
+                    start=True,
+                    stop=True,
+                )
+            live = min(CHUNK, MADE_TOKENS - c * CHUNK)
+            nc.scalar.copy(
+                out=diffs[k][:, :, c * CHUNK : c * CHUNK + live, :],
+                in_=made[:, :, :, :live].rearrange("p t s n -> p s n t"),
+            )
+
         def subtract(k):
-            diff = diff_pool.tile([P, SOURCES, PAIR_TOKENS, PACK], BF16, align_bytes=64)
-            ve_shape = [P, SOURCES, VE_TOKENS, PACK]
-            gp_shape = [P, SOURCES, GP_TOKENS, PACK]
+            if k in MADE_PAIRS:
+                diff = diffs[k]
+                first, gp_tokens = MADE_TOKENS, GP_TOKENS_MADE
+            else:
+                diff = diff_pool.tile([P, SOURCES, PAIR_TOKENS, PACK], BF16, align_bytes=64)
+                diffs[k] = diff
+                first, gp_tokens = 0, GP_TOKENS
+            last = PAIR_TOKENS - gp_tokens
+            ve_shape = [P, SOURCES, last - first, PACK]
+            gp_shape = [P, SOURCES, gp_tokens, PACK]
             nc.gpsimd.tensor_tensor(
-                out=diff[:, :, VE_TOKENS:, :],
+                out=diff[:, :, last:, :],
                 in0=sides[k][:].unsqueeze(1).to_broadcast(gp_shape),
                 in1=dom_t[:].unsqueeze(2).to_broadcast(gp_shape),
                 op=ALU.subtract,
             )
             nc.vector.tensor_tensor(
-                out=diff[:, :, :VE_TOKENS, :],
-                in0=turneds[k][:, :VE_TOKENS, :].bitcast(BF16).unsqueeze(1).to_broadcast(ve_shape),
+                out=diff[:, :, first:last, :],
+                in0=turneds[k][:, first:last, :].bitcast(BF16).unsqueeze(1).to_broadcast(ve_shape),
                 in1=dom_t[:].unsqueeze(2).to_broadcast(ve_shape),
                 op=ALU.subtract,
             )
-            diffs[k] = diff
 
         def project(k):
             codes = mx_pool.tile([P, SOURCES, PAIR_TOKENS], U32, align_bytes=64)
@@ -157,6 +207,9 @@ def tile_moe_pa_e_kernel(tc, encodings, domain_encs, Us_words, Us_scales, out):
                 subtract(k + 1)
             if k + AHEAD < PAIRS:
                 turn(k + AHEAD)
+            for made_k in MADE_PAIRS:
+                if 0 <= k - (made_k - 1 - CHUNKS) < CHUNKS:
+                    make(made_k, k - (made_k - 1 - CHUNKS))
             project(k)
 
         by_token = "p s j -> p j s"

@@ -23,34 +23,39 @@ HALVES = 2
 QUADRANT = 32
 LIVE_ROWS = 4
 TILES = TOKENS // P
-PAIR = 2
-PAIRS = TILES // PAIR
-PAIR_TOKENS = PAIR * P
+EDGE_SINGLES = 0
 AHEAD = 2
 PROJ_BANKS = 4
 MADE_BANKS = 2
-GP_TOKENS = 40
-MADE_PAIRS = (6, 10, 14)
+GP_TOKENS = 20
+MADE_GROUPS = (6, 10, 14)
 MADE_TOKENS = P - SOURCES
 CHUNK = 32
 CHUNKS = P // CHUNK
-GP_TOKENS_MADE = 20
 
 FLOPS = 2 * SOURCES * TOKENS * HIDDEN * RANK
 
 
+def token_groups():
+    groups = [(j,) for j in range(EDGE_SINGLES)]
+    groups.extend([(j, j + 1) for j in range(EDGE_SINGLES, TILES - EDGE_SINGLES, 2)])
+    groups.extend([(j,) for j in range(TILES - EDGE_SINGLES, TILES)])
+    return groups
+
+
 def tile_moe_pa_e_kernel(tc, encodings, domain_encs, Us_words, Us_scales, out):
     nc = tc.nc
+    groups = token_groups()
     with ExitStack() as ctx:
         keep = ctx.enter_context(tc.tile_pool(name="keep", bufs=1))
         side_pool = ctx.enter_context(tc.tile_pool(name="side_pool", bufs=AHEAD))
         diff_pool = ctx.enter_context(tc.tile_pool(name="diff_pool", bufs=2))
-        mx_pool = ctx.enter_context(tc.tile_pool(name="mx_pool", bufs=3))
+        made_pool = ctx.enter_context(tc.tile_pool(name="made_pool", bufs=2))
+        mx_pool = ctx.enter_context(tc.tile_pool(name="mx_pool", bufs=4))
         square_pool = ctx.enter_context(tc.tile_pool(name="square_pool", bufs=PROJ_BANKS))
         turned_psum = ctx.enter_context(tc.psum_pool(name="turned_psum", bufs=AHEAD))
         proj_psum = ctx.enter_context(tc.psum_pool(name="proj_psum", bufs=PROJ_BANKS))
         made_psum = ctx.enter_context(tc.psum_pool(name="made_psum", bufs=MADE_BANKS))
-        made_pool = ctx.enter_context(tc.tile_pool(name="made_pool", bufs=2))
 
         enc_rows = encodings.rearrange("(p j) h -> p j h", j=TILES)
         enc_sb = keep.tile([P, TILES, HIDDEN], BF16)
@@ -71,8 +76,7 @@ def tile_moe_pa_e_kernel(tc, encodings, domain_encs, Us_words, Us_scales, out):
         ident = keep.tile([P, P], F32)
         make_identity(nc, ident[:])
 
-        for j in range(1, PAIR):
-            load_tokens(j)
+        load_tokens(1)
 
         u_codes = keep.tile([P, SOURCES, RANK], U32, align_bytes=64)
         nc.sync.dma_start(
@@ -97,91 +101,93 @@ def tile_moe_pa_e_kernel(tc, encodings, domain_encs, Us_words, Us_scales, out):
         )
         augs = {}
 
-        def load_made(k):
-            aug = keep.tile([P, HIDDEN], BF16, name="aug%d" % k)
-            nc.sync.dma_start(out=aug[:MADE_TOKENS, :], in_=enc_rows[:MADE_TOKENS, PAIR * k, :])
+        def load_made(g):
+            aug = keep.tile([P, HIDDEN], BF16, name="aug%d" % g)
+            nc.sync.dma_start(out=aug[:MADE_TOKENS, :], in_=enc_rows[:MADE_TOKENS, groups[g][0], :])
             nc.sync.dma_start(out=aug[MADE_TOKENS:, :], in_=domain_encs)
-            augs[k] = aug
+            augs[g] = aug
 
-        for j in range(PAIR, TILES):
-            if j % PAIR == 0 and (j // PAIR + 2) in MADE_PAIRS:
-                load_made(j // PAIR + 2)
-            load_tokens(j)
+        for g in range(len(groups)):
+            if g + 2 in MADE_GROUPS:
+                load_made(g + 2)
+            for j in groups[g]:
+                if j > 1:
+                    load_tokens(j)
 
         sumsq = keep.tile([P, SOURCES, TILES], F32)
         turneds = {}
         sides = {}
         diffs = {}
+        made_diffs = {}
 
-        def turn(k):
-            turned = turned_psum.tile([P, PAIR_TOKENS, HALVES], F32)
-            for h in range(PAIR):
-                words = enc_sb[:, PAIR * k + h, :].bitcast(F32)
+        def gp_tokens(g):
+            return GP_TOKENS * (len(groups[g]) - (1 if g in MADE_GROUPS else 0))
+
+        def turn(g):
+            tokens = len(groups[g]) * P
+            turned = turned_psum.tile([P, tokens, HALVES], F32)
+            for i, j in enumerate(groups[g]):
+                words = enc_sb[:, j, :].bitcast(F32)
                 for u in range(HALVES):
                     nc.tensor.transpose(
-                        out=turned[:, h * P : (h + 1) * P, u],
+                        out=turned[:, i * P : (i + 1) * P, u],
                         in_=words[:, u : HIDDEN // 2 : HALVES],
                         identity=ident[:],
                     )
-            turneds[k] = turned
-            gp_tokens = GP_TOKENS_MADE if k in MADE_PAIRS else GP_TOKENS
-            side = side_pool.tile([P, gp_tokens, PACK], BF16)
-            nc.scalar.copy(out=side[:].bitcast(F32), in_=turned[:, PAIR_TOKENS - gp_tokens :, :])
-            sides[k] = side
+            turneds[g] = turned
+            side = side_pool.tile([P, gp_tokens(g), PACK], BF16)
+            nc.scalar.copy(out=side[:].bitcast(F32), in_=turned[:, tokens - gp_tokens(g) :, :])
+            sides[g] = side
 
-        def make(k, c):
+        def make(g, c):
             if c == 0:
-                diffs[k] = made_pool.tile([P, SOURCES, PAIR_TOKENS, PACK], BF16, align_bytes=64, name="made_diff")
+                made_diffs[g] = made_pool.tile([P, SOURCES, P, PACK], BF16, align_bytes=64, name="made_diff")
             made = made_psum.tile([P, PACK, SOURCES, CHUNK], F32)
             for t in range(PACK):
                 nc.tensor.matmul(
                     out=made[:, t, :, :].rearrange("p s n -> p (s n)"),
-                    lhsT=augs[k][:, t:HIDDEN:PACK],
+                    lhsT=augs[g][:, t:HIDDEN:PACK],
                     rhs=sel[:, c, :, :].rearrange("p s n -> p (s n)"),
                     start=True,
                     stop=True,
                 )
             live = min(CHUNK, MADE_TOKENS - c * CHUNK)
             nc.scalar.copy(
-                out=diffs[k][:, :, c * CHUNK : c * CHUNK + live, :],
+                out=made_diffs[g][:, :, c * CHUNK : c * CHUNK + live, :],
                 in_=made[:, :, :, :live].rearrange("p t s n -> p s n t"),
             )
 
-        def subtract(k):
-            if k in MADE_PAIRS:
-                diff = diffs[k]
-                first, gp_tokens = MADE_TOKENS, GP_TOKENS_MADE
-            else:
-                diff = diff_pool.tile([P, SOURCES, PAIR_TOKENS, PACK], BF16, align_bytes=64)
-                diffs[k] = diff
-                first, gp_tokens = 0, GP_TOKENS
-            last = PAIR_TOKENS - gp_tokens
-            ve_shape = [P, SOURCES, last - first, PACK]
-            gp_shape = [P, SOURCES, gp_tokens, PACK]
-            nc.gpsimd.tensor_tensor(
-                out=diff[:, :, last:, :],
-                in0=sides[k][:].unsqueeze(1).to_broadcast(gp_shape),
-                in1=dom_t[:].unsqueeze(2).to_broadcast(gp_shape),
-                op=ALU.subtract,
-            )
-            nc.vector.tensor_tensor(
-                out=diff[:, :, first:last, :],
-                in0=turneds[k][:, first:last, :].bitcast(BF16).unsqueeze(1).to_broadcast(ve_shape),
-                in1=dom_t[:].unsqueeze(2).to_broadcast(ve_shape),
+        def minus(engine, diff, tokens):
+            shape = [P, SOURCES, tokens.shape[1], PACK]
+            engine.tensor_tensor(
+                out=diff,
+                in0=tokens.unsqueeze(1).to_broadcast(shape),
+                in1=dom_t[:].unsqueeze(2).to_broadcast(shape),
                 op=ALU.subtract,
             )
 
-        def project(k):
-            codes = mx_pool.tile([P, SOURCES, PAIR_TOKENS], U32, align_bytes=64)
-            scales = mx_pool.tile([P, SOURCES, PAIR_TOKENS], U8, align_bytes=64)
+        def subtract(g):
+            first = P if g in MADE_GROUPS else 0
+            width = len(groups[g]) * P - first
+            ve_tokens = width - gp_tokens(g)
+            diff = diff_pool.tile([P, SOURCES, width, PACK], BF16, align_bytes=64)
+            diffs[g] = diff
+            as_bf16 = turneds[g][:].bitcast(BF16)
+            minus(nc.gpsimd, diff[:, :, ve_tokens:, :], sides[g][:])
+            minus(nc.vector, diff[:, :, :ve_tokens, :], as_bf16[:, first : first + ve_tokens, :])
+            if g in MADE_GROUPS:
+                minus(nc.vector, made_diffs[g][:, :, MADE_TOKENS:, :], as_bf16[:, MADE_TOKENS:P, :])
+
+        def project(diff, tiles):
+            codes = mx_pool.tile([P, SOURCES, len(tiles) * P], U32, align_bytes=64)
+            scales = mx_pool.tile([P, SOURCES, len(tiles) * P], U8, align_bytes=64)
             nc.vector.quantize_mx(
                 out=codes[:].rearrange("p s n -> p (s n)").bitcast(FP8X4),
                 scales=scales[:].rearrange("p s n -> p (s n)"),
-                in_=diffs[k][:].rearrange("p s n t -> p (s n t)"),
+                in_=diff[:].rearrange("p s n t -> p (s n t)"),
             )
-            for h in range(PAIR):
-                j = PAIR * k + h
-                tokens = slice(h * P, (h + 1) * P)
+            for i, j in enumerate(tiles):
+                tokens = slice(i * P, (i + 1) * P)
                 proj = proj_psum.tile([P, SOURCES, RANK], F32)
                 for s in range(SOURCES):
                     nc.tensor.matmul_mx(
@@ -199,18 +205,22 @@ def tile_moe_pa_e_kernel(tc, encodings, domain_encs, Us_words, Us_scales, out):
                         out=squares[:, s, :], in_=proj[:, s, :], func=ACT.Square, accum_out=sumsq[:, s, j : j + 1]
                     )
 
-        for k in range(AHEAD):
-            turn(k)
+        for g in range(AHEAD):
+            turn(g)
         subtract(0)
-        for k in range(PAIRS):
-            if k + 1 < PAIRS:
-                subtract(k + 1)
-            if k + AHEAD < PAIRS:
-                turn(k + AHEAD)
-            for made_k in MADE_PAIRS:
-                if 0 <= k - (made_k - 1 - CHUNKS) < CHUNKS:
-                    make(made_k, k - (made_k - 1 - CHUNKS))
-            project(k)
+        for g in range(len(groups)):
+            if g + 1 < len(groups):
+                subtract(g + 1)
+            if g + AHEAD < len(groups):
+                turn(g + AHEAD)
+            for made_g in MADE_GROUPS:
+                if 0 <= g - (made_g - 1 - CHUNKS) < CHUNKS:
+                    make(made_g, g - (made_g - 1 - CHUNKS))
+            if g in MADE_GROUPS:
+                project(made_diffs[g], groups[g][:1])
+                project(diffs[g], groups[g][1:])
+            else:
+                project(diffs[g], groups[g])
 
         by_token = "p s j -> p j s"
         spread = [P, SOURCES, TILES]

@@ -23,13 +23,13 @@ HALVES = 2
 QUADRANT = 32
 LIVE_ROWS = 4
 TILES = TOKENS // P
-EDGE_SINGLES = 0
+EDGE_SINGLES = 2
 AHEAD = 2
 PROJ_BANKS = 4
 MADE_BANKS = 2
 GP_TOKENS = 20
-MADE_GROUPS = (6, 10, 14)
-MADE_TOKENS = P - SOURCES
+MADE_GROUPS = (7, 11, 15)
+TOKEN_ROWS = P - SOURCES
 CHUNK = 32
 CHUNKS = P // CHUNK
 
@@ -92,25 +92,38 @@ def tile_moe_pa_e_kernel(tc, encodings, domain_encs, Us_words, Us_scales, out):
             )
 
         sel = keep.tile([P, CHUNKS, SOURCES, CHUNK], BF16)
-        sel_shape = [P, CHUNKS, SOURCES, CHUNK]
-        nc.vector.tensor_tensor(
-            out=sel[:],
-            in0=ident[:].rearrange("p (c n) -> p c n", n=CHUNK).unsqueeze(2).to_broadcast(sel_shape),
-            in1=ident[:, MADE_TOKENS:].unsqueeze(1).unsqueeze(3).to_broadcast(sel_shape),
+        low_shape = [P, CHUNKS - 1, SOURCES, CHUNK]
+        nc.gpsimd.tensor_tensor(
+            out=sel[:, : CHUNKS - 1, :, :],
+            in0=ident[:, : P - CHUNK].rearrange("p (c n) -> p c n", n=CHUNK).unsqueeze(2).to_broadcast(low_shape),
+            in1=ident[:, TOKEN_ROWS:].unsqueeze(1).unsqueeze(3).to_broadcast(low_shape),
+            op=ALU.subtract,
+        )
+        high_shape = [P, SOURCES, CHUNK]
+        nc.gpsimd.tensor_tensor(
+            out=sel[:, CHUNKS - 1, :, :],
+            in0=ident[:, TOKEN_ROWS - CHUNK : TOKEN_ROWS].unsqueeze(1).to_broadcast(high_shape),
+            in1=ident[:, TOKEN_ROWS:].unsqueeze(2).to_broadcast(high_shape),
             op=ALU.subtract,
         )
         augs = {}
 
+        def subtracted(g):
+            return groups[g][1:] if g in MADE_GROUPS else groups[g]
+
         def load_made(g):
-            aug = keep.tile([P, HIDDEN], BF16, name="aug%d" % g)
-            nc.sync.dma_start(out=aug[:MADE_TOKENS, :], in_=enc_rows[:MADE_TOKENS, groups[g][0], :])
-            nc.sync.dma_start(out=aug[MADE_TOKENS:, :], in_=domain_encs)
-            augs[g] = aug
+            low = keep.tile([P, HIDDEN], BF16, name="low%d" % g)
+            high = keep.tile([P, HIDDEN], BF16, name="high%d" % g)
+            nc.sync.dma_start(out=low[:TOKEN_ROWS, :], in_=enc_rows[:TOKEN_ROWS, groups[g][0], :])
+            nc.sync.dma_start(out=low[TOKEN_ROWS:, :], in_=domain_encs)
+            nc.sync.dma_start(out=high[:TOKEN_ROWS, :], in_=enc_rows[SOURCES:, groups[g][0], :])
+            nc.sync.dma_start(out=high[TOKEN_ROWS:, :], in_=domain_encs)
+            augs[g] = (low, high)
 
         for g in range(len(groups)):
             if g + 2 in MADE_GROUPS:
                 load_made(g + 2)
-            for j in groups[g]:
+            for j in subtracted(g):
                 if j > 1:
                     load_tokens(j)
 
@@ -121,12 +134,13 @@ def tile_moe_pa_e_kernel(tc, encodings, domain_encs, Us_words, Us_scales, out):
         made_diffs = {}
 
         def gp_tokens(g):
-            return GP_TOKENS * (len(groups[g]) - (1 if g in MADE_GROUPS else 0))
+            return GP_TOKENS * len(subtracted(g))
 
         def turn(g):
-            tokens = len(groups[g]) * P
+            tiles = subtracted(g)
+            tokens = len(tiles) * P
             turned = turned_psum.tile([P, tokens, HALVES], F32)
-            for i, j in enumerate(groups[g]):
+            for i, j in enumerate(tiles):
                 words = enc_sb[:, j, :].bitcast(F32)
                 for u in range(HALVES):
                     nc.tensor.transpose(
@@ -143,18 +157,18 @@ def tile_moe_pa_e_kernel(tc, encodings, domain_encs, Us_words, Us_scales, out):
             if c == 0:
                 made_diffs[g] = made_pool.tile([P, SOURCES, P, PACK], BF16, align_bytes=64, name="made_diff")
             made = made_psum.tile([P, PACK, SOURCES, CHUNK], F32)
+            aug = augs[g][1 if c == CHUNKS - 1 else 0]
             for t in range(PACK):
                 nc.tensor.matmul(
                     out=made[:, t, :, :].rearrange("p s n -> p (s n)"),
-                    lhsT=augs[g][:, t:HIDDEN:PACK],
+                    lhsT=aug[:, t:HIDDEN:PACK],
                     rhs=sel[:, c, :, :].rearrange("p s n -> p (s n)"),
                     start=True,
                     stop=True,
                 )
-            live = min(CHUNK, MADE_TOKENS - c * CHUNK)
             nc.scalar.copy(
-                out=made_diffs[g][:, :, c * CHUNK : c * CHUNK + live, :],
-                in_=made[:, :, :, :live].rearrange("p t s n -> p s n t"),
+                out=made_diffs[g][:, :, c * CHUNK : (c + 1) * CHUNK, :],
+                in_=made[:].rearrange("p t s n -> p s n t"),
             )
 
         def minus(engine, diff, tokens):
@@ -167,16 +181,13 @@ def tile_moe_pa_e_kernel(tc, encodings, domain_encs, Us_words, Us_scales, out):
             )
 
         def subtract(g):
-            first = P if g in MADE_GROUPS else 0
-            width = len(groups[g]) * P - first
+            width = len(subtracted(g)) * P
             ve_tokens = width - gp_tokens(g)
             diff = diff_pool.tile([P, SOURCES, width, PACK], BF16, align_bytes=64)
             diffs[g] = diff
             as_bf16 = turneds[g][:].bitcast(BF16)
             minus(nc.gpsimd, diff[:, :, ve_tokens:, :], sides[g][:])
-            minus(nc.vector, diff[:, :, :ve_tokens, :], as_bf16[:, first : first + ve_tokens, :])
-            if g in MADE_GROUPS:
-                minus(nc.vector, made_diffs[g][:, :, MADE_TOKENS:, :], as_bf16[:, MADE_TOKENS:P, :])
+            minus(nc.vector, diff[:, :, :ve_tokens, :], as_bf16[:, :ve_tokens, :])
 
         def project(diff, tiles):
             codes = mx_pool.tile([P, SOURCES, len(tiles) * P], U32, align_bytes=64)

@@ -24,9 +24,9 @@ QUADRANT = 32
 LIVE_ROWS = 4
 TILES = TOKENS // P
 EDGE_SINGLES = 2
-AHEAD = 2
+AHEAD = 3
 PROJ_BANKS = 4
-MADE_BANKS = 2
+MADE_BANKS = 1
 GP_TOKENS = 20
 MADE_GROUPS = (7, 11, 15)
 TOKEN_ROWS = P - SOURCES
@@ -216,6 +216,30 @@ def tile_moe_pa_e_kernel(tc, encodings, domain_encs, Us_words, Us_scales, out):
                         out=squares[:, s, :], in_=proj[:, s, :], func=ACT.Square, accum_out=sumsq[:, s, j : j + 1]
                     )
 
+        def project_by_source(diff, j):
+            codes = mx_pool.tile([P, SOURCES, P], U32, align_bytes=64)
+            scales = mx_pool.tile([P, SOURCES, P], U8, align_bytes=64)
+            squares = square_pool.tile([P, SOURCES, RANK], F32)
+            for s in range(SOURCES):
+                nc.vector.quantize_mx(
+                    out=codes[:, s, :].bitcast(FP8X4),
+                    scales=scales[:, s, :],
+                    in_=diff[:, s, :, :].rearrange("p n t -> p (n t)"),
+                )
+                proj = proj_psum.tile([P, RANK], F32)
+                nc.tensor.matmul_mx(
+                    out=proj[:],
+                    lhsT=codes[:, s, :].bitcast(FP8X4),
+                    lhsT_scale=scales[:, s, :],
+                    rhs=u_codes[:, s, :].bitcast(FP8X4),
+                    rhs_scale=u_scales[:, s, :],
+                    start=True,
+                    stop=True,
+                )
+                nc.scalar.activation(
+                    out=squares[:, s, :], in_=proj[:], func=ACT.Square, accum_out=sumsq[:, s, j : j + 1]
+                )
+
         for g in range(AHEAD):
             turn(g)
         subtract(0)
@@ -230,8 +254,10 @@ def tile_moe_pa_e_kernel(tc, encodings, domain_encs, Us_words, Us_scales, out):
             if g in MADE_GROUPS:
                 project(made_diffs[g], groups[g][:1])
                 project(diffs[g], groups[g][1:])
-            else:
+            elif g + 1 < len(groups):
                 project(diffs[g], groups[g])
+            else:
+                project_by_source(diffs[g], groups[g][0])
 
         by_token = "p s j -> p j s"
         spread = [P, SOURCES, TILES]
@@ -246,11 +272,22 @@ def tile_moe_pa_e_kernel(tc, encodings, domain_encs, Us_words, Us_scales, out):
         weight = keep.tile(spread, F32)
         nc.scalar.activation(out=weight[:], in_=excess[:], func=ACT.Exp, scale=-1.0)
         total = keep.tile([P, TILES], F32)
-        nc.vector.tensor_reduce(out=total[:], in_=weight[:].rearrange(by_token), axis=AXIS.X, op=ALU.add)
         inverse = keep.tile([P, TILES], F32)
-        nc.vector.reciprocal(out=inverse[:], in_=total[:])
         alphas = keep.tile(spread, F32)
-        nc.vector.tensor_tensor(
-            out=alphas[:], in0=weight[:], in1=inverse[:].unsqueeze(1).to_broadcast(spread), op=ALU.mult
-        )
-        nc.sync.dma_start(out=out.rearrange("s (p j) -> p s j", j=TILES), in_=alphas[:])
+        halves = (slice(0, TILES // 2), slice(TILES // 2, TILES))
+        half_spread = [P, SOURCES, TILES // 2]
+        for half in halves:
+            nc.vector.tensor_reduce(
+                out=total[:, half], in_=weight[:, :, half].rearrange(by_token), axis=AXIS.X, op=ALU.add
+            )
+        for half in halves:
+            nc.vector.reciprocal(out=inverse[:, half], in_=total[:, half])
+        out_by_tile = out.rearrange("s (p j) -> p s j", j=TILES)
+        for half, queue in zip(halves, (nc.sync, nc.scalar)):
+            nc.vector.tensor_tensor(
+                out=alphas[:, :, half],
+                in0=weight[:, :, half],
+                in1=inverse[:, half].unsqueeze(1).to_broadcast(half_spread),
+                op=ALU.mult,
+            )
+            queue.dma_start(out=out_by_tile[:, :, half], in_=alphas[:, :, half])

@@ -27,7 +27,7 @@ EDGE_SINGLES = 2
 AHEAD = 3
 PROJ_BANKS = 4
 MADE_BANKS = 1
-GP_TOKENS = 20
+GP_TOKENS = (0, 20, 44)
 MADE_GROUPS = (7, 11, 15)
 TOKEN_ROWS = P - SOURCES
 CHUNK = 32
@@ -134,7 +134,7 @@ def tile_moe_pa_e_kernel(tc, encodings, domain_encs, Us_words, Us_scales, out):
         made_diffs = {}
 
         def gp_tokens(g):
-            return GP_TOKENS * len(subtracted(g))
+            return GP_TOKENS[len(subtracted(g))]
 
         def turn(g):
             tiles = subtracted(g)

@@ -24,6 +24,7 @@ QUADRANT = 32
 LIVE_ROWS = 4
 TILES = TOKENS // P
 EDGE_SINGLES = 2
+EARLY_TILES = 4
 AHEAD = 3
 PROJ_BANKS = 4
 MADE_BANKS = 1
@@ -76,7 +77,8 @@ def tile_moe_pa_e_kernel(tc, encodings, domain_encs, Us_words, Us_scales, out):
         ident = keep.tile([P, P], F32)
         make_identity(nc, ident[:])
 
-        load_tokens(1)
+        for j in range(1, EARLY_TILES):
+            load_tokens(j)
 
         u_codes = keep.tile([P, SOURCES, RANK], U32, align_bytes=64)
         nc.sync.dma_start(
@@ -124,10 +126,11 @@ def tile_moe_pa_e_kernel(tc, encodings, domain_encs, Us_words, Us_scales, out):
             if g + 2 in MADE_GROUPS:
                 load_made(g + 2)
             for j in subtracted(g):
-                if j > 1:
+                if j >= EARLY_TILES:
                     load_tokens(j)
 
         sumsq = keep.tile([P, SOURCES, TILES], F32)
+        dist = keep.tile([P, SOURCES, TILES], F32)
         turneds = {}
         sides = {}
         diffs = {}
@@ -251,6 +254,8 @@ def tile_moe_pa_e_kernel(tc, encodings, domain_encs, Us_words, Us_scales, out):
             for made_g in MADE_GROUPS:
                 if 0 <= g - (made_g - 1 - CHUNKS) < CHUNKS:
                     make(made_g, g - (made_g - 1 - CHUNKS))
+            if g == len(groups) - EDGE_SINGLES:
+                nc.scalar.activation(out=dist[:, :, : groups[g][0]], in_=sumsq[:, :, : groups[g][0]], func=ACT.Sqrt)
             if g in MADE_GROUPS:
                 project(made_diffs[g], groups[g][:1])
                 project(diffs[g], groups[g][1:])
@@ -261,8 +266,8 @@ def tile_moe_pa_e_kernel(tc, encodings, domain_encs, Us_words, Us_scales, out):
 
         by_token = "p s j -> p j s"
         spread = [P, SOURCES, TILES]
-        dist = keep.tile(spread, F32)
-        nc.scalar.activation(out=dist[:], in_=sumsq[:], func=ACT.Sqrt)
+        late = slice(TILES - EDGE_SINGLES, TILES)
+        nc.scalar.activation(out=dist[:, :, late], in_=sumsq[:, :, late], func=ACT.Sqrt)
         nearest = keep.tile([P, TILES], F32)
         nc.vector.tensor_reduce(out=nearest[:], in_=dist[:].rearrange(by_token), axis=AXIS.X, op=ALU.min)
         excess = keep.tile(spread, F32)

@@ -26,10 +26,13 @@ TILES = TOKENS // P
 EDGE_SINGLES = 2
 EARLY_TILES = 4
 AHEAD = 3
-PROJ_BANKS = 4
-MADE_BANKS = 1
+PROJ_BANKS = 3
+MADE_BANKS = 2
 GP_TOKENS = (0, 20, 44)
-MADE_GROUPS = (7, 11, 15)
+PLAIN_GROUPS = (7, 10, 15)
+SUMMED_GROUPS = (12,)
+MADE_GROUPS = tuple(sorted(PLAIN_GROUPS + SUMMED_GROUPS))
+FIRST_PIECE_STEP = 2
 TOKEN_ROWS = P - SOURCES
 CHUNK = 32
 CHUNKS = P // CHUNK
@@ -51,7 +54,8 @@ def tile_moe_pa_e_kernel(tc, encodings, domain_encs, Us_words, Us_scales, out):
         keep = ctx.enter_context(tc.tile_pool(name="keep", bufs=1))
         side_pool = ctx.enter_context(tc.tile_pool(name="side_pool", bufs=AHEAD))
         diff_pool = ctx.enter_context(tc.tile_pool(name="diff_pool", bufs=2))
-        made_pool = ctx.enter_context(tc.tile_pool(name="made_pool", bufs=2))
+        made_pool = ctx.enter_context(tc.tile_pool(name="made_pool", bufs=3))
+        wide_pool = ctx.enter_context(tc.tile_pool(name="wide_pool", bufs=2))
         mx_pool = ctx.enter_context(tc.tile_pool(name="mx_pool", bufs=4))
         square_pool = ctx.enter_context(tc.tile_pool(name="square_pool", bufs=PROJ_BANKS))
         turned_psum = ctx.enter_context(tc.psum_pool(name="turned_psum", bufs=AHEAD))
@@ -123,8 +127,10 @@ def tile_moe_pa_e_kernel(tc, encodings, domain_encs, Us_words, Us_scales, out):
             augs[g] = (low, high)
 
         for g in range(len(groups)):
-            if g + 2 in MADE_GROUPS:
-                load_made(g + 2)
+            if g + 3 in PLAIN_GROUPS:
+                load_made(g + 3)
+            if g + 4 in SUMMED_GROUPS:
+                load_tokens(groups[g + 4][0])
             for j in subtracted(g):
                 if j >= EARLY_TILES:
                     load_tokens(j)
@@ -173,6 +179,35 @@ def tile_moe_pa_e_kernel(tc, encodings, domain_encs, Us_words, Us_scales, out):
                 out=made_diffs[g][:, :, c * CHUNK : (c + 1) * CHUNK, :],
                 in_=made[:].rearrange("p t s n -> p s n t"),
             )
+
+        neg_t = keep.tile([P, SOURCES, PACK], F32)
+        neg_dom = keep.tile([P, SOURCES, PACK, P], F32)
+        wides = {}
+
+        def spread_dom(s):
+            made = made_psum.tile([P, PACK, P], F32)
+            for t in range(PACK):
+                nc.tensor.transpose(
+                    out=made[:, t, :], in_=neg_t[:, s, t : t + 1].to_broadcast([P, P]), identity=ident[:]
+                )
+            nc.scalar.copy(out=neg_dom[:, s, :, :], in_=made[:])
+
+        def widen(g, unused):
+            made_diffs[g] = made_pool.tile([P, SOURCES, P, PACK], BF16, align_bytes=64, name="made_diff")
+            wide = wide_pool.tile([P, PACK, P], F32)
+            nc.scalar.copy(out=wide[:], in_=enc_sb[:, groups[g][0], :].rearrange("n (p t) -> n t p", t=PACK))
+            wides[g] = wide
+
+        def add_up(g, s):
+            made = made_psum.tile([P, PACK, P], F32)
+            for t in range(PACK):
+                nc.tensor.matmul(
+                    out=made[:, t, :], lhsT=neg_dom[:, s, t, :], rhs=ident[:], is_transpose=True, start=True, stop=False
+                )
+                nc.tensor.matmul(
+                    out=made[:, t, :], lhsT=wides[g][:, t, :], rhs=ident[:], is_transpose=True, start=False, stop=True
+                )
+            nc.scalar.copy(out=made_diffs[g][:, s, :, :], in_=made[:].rearrange("p t n -> p n t"))
 
         def minus(engine, diff, tokens):
             shape = [P, SOURCES, tokens.shape[1], PACK]
@@ -243,17 +278,29 @@ def tile_moe_pa_e_kernel(tc, encodings, domain_encs, Us_words, Us_scales, out):
                     out=squares[:, s, :], in_=proj[:], func=ACT.Square, accum_out=sumsq[:, s, j : j + 1]
                 )
 
+        pieces = []
+        for made_g in MADE_GROUPS:
+            if made_g in SUMMED_GROUPS:
+                pieces.append((widen, made_g, 0))
+                pieces.extend([(add_up, made_g, s) for s in range(SOURCES)])
+            else:
+                pieces.extend([(make, made_g, c) for c in range(CHUNKS)])
+        piece_steps = MADE_GROUPS[-1] - 1 - FIRST_PIECE_STEP
         for g in range(AHEAD):
             turn(g)
         subtract(0)
+        nc.scalar.activation(out=neg_t[:], in_=dom_t[:], func=ACT.Copy, scale=-1.0)
+        for s in range(SOURCES):
+            spread_dom(s)
         for g in range(len(groups)):
             if g + 1 < len(groups):
                 subtract(g + 1)
             if g + AHEAD < len(groups):
                 turn(g + AHEAD)
-            for made_g in MADE_GROUPS:
-                if 0 <= g - (made_g - 1 - CHUNKS) < CHUNKS:
-                    make(made_g, g - (made_g - 1 - CHUNKS))
+            for q, piece in enumerate(pieces):
+                if FIRST_PIECE_STEP + q * piece_steps // len(pieces) == g:
+                    assert g <= piece[1] - 2
+                    piece[0](piece[1], piece[2])
             if g == len(groups) - EDGE_SINGLES:
                 nc.scalar.activation(out=dist[:, :, : groups[g][0]], in_=sumsq[:, :, : groups[g][0]], func=ACT.Sqrt)
             if g in MADE_GROUPS:

@@ -24,15 +24,19 @@ QUADRANT = 32
 LIVE_ROWS = 4
 TILES = TOKENS // P
 EDGE_SINGLES = 2
+BATCH = 2
+FINE_GROUPS = 6
+LATE_TILES = 6
 EARLY_TILES = 4
 AHEAD = 3
 PROJ_BANKS = 3
 MADE_BANKS = 2
 GP_TOKENS = (0, 20, 44)
-PLAIN_GROUPS = (7, 10, 15)
-SUMMED_GROUPS = (12,)
+PLAIN_GROUPS = (7, 11, 15)
+SUMMED_GROUPS = (9, 13)
 MADE_GROUPS = tuple(sorted(PLAIN_GROUPS + SUMMED_GROUPS))
 FIRST_PIECE_STEP = 2
+MADE_AHEAD = 4
 TOKEN_ROWS = P - SOURCES
 CHUNK = 32
 CHUNKS = P // CHUNK
@@ -51,12 +55,13 @@ def tile_moe_pa_e_kernel(tc, encodings, domain_encs, Us_words, Us_scales, out):
     nc = tc.nc
     groups = token_groups()
     with ExitStack() as ctx:
+        ctx.enter_context(tc.manual_schedule(engines={mybir.EngineType.DVE, mybir.EngineType.Pool}))
         keep = ctx.enter_context(tc.tile_pool(name="keep", bufs=1))
         side_pool = ctx.enter_context(tc.tile_pool(name="side_pool", bufs=AHEAD))
         diff_pool = ctx.enter_context(tc.tile_pool(name="diff_pool", bufs=2))
-        made_pool = ctx.enter_context(tc.tile_pool(name="made_pool", bufs=3))
+        made_pool = ctx.enter_context(tc.tile_pool(name="made_pool", bufs=5))
         wide_pool = ctx.enter_context(tc.tile_pool(name="wide_pool", bufs=2))
-        mx_pool = ctx.enter_context(tc.tile_pool(name="mx_pool", bufs=4))
+        mx_pool = ctx.enter_context(tc.tile_pool(name="mx_pool", bufs=8))
         square_pool = ctx.enter_context(tc.tile_pool(name="square_pool", bufs=PROJ_BANKS))
         turned_psum = ctx.enter_context(tc.psum_pool(name="turned_psum", bufs=AHEAD))
         proj_psum = ctx.enter_context(tc.psum_pool(name="proj_psum", bufs=PROJ_BANKS))
@@ -209,74 +214,75 @@ def tile_moe_pa_e_kernel(tc, encodings, domain_encs, Us_words, Us_scales, out):
                 )
             nc.scalar.copy(out=made_diffs[g][:, s, :, :], in_=made[:].rearrange("p t n -> p n t"))
 
-        def minus(engine, diff, tokens):
-            shape = [P, SOURCES, tokens.shape[1], PACK]
+        every_source = slice(0, SOURCES)
+
+        def minus(engine, diff, tokens, sources=every_source):
+            shape = [P, sources.stop - sources.start, tokens.shape[1], PACK]
             engine.tensor_tensor(
-                out=diff,
+                out=diff[:, sources, :, :],
                 in0=tokens.unsqueeze(1).to_broadcast(shape),
-                in1=dom_t[:].unsqueeze(2).to_broadcast(shape),
+                in1=dom_t[:, sources, :].unsqueeze(2).to_broadcast(shape),
                 op=ALU.subtract,
             )
 
-        def subtract(g):
+        def subtract(g, parts=(every_source,)):
             width = len(subtracted(g)) * P
             ve_tokens = width - gp_tokens(g)
             diff = diff_pool.tile([P, SOURCES, width, PACK], BF16, align_bytes=64)
             diffs[g] = diff
             as_bf16 = turneds[g][:].bitcast(BF16)
             minus(nc.gpsimd, diff[:, :, ve_tokens:, :], sides[g][:])
-            minus(nc.vector, diff[:, :, :ve_tokens, :], as_bf16[:, :ve_tokens, :])
+            for part in parts:
+                minus(nc.vector, diff[:, :, :ve_tokens, :], as_bf16[:, :ve_tokens, :], part)
+
+        def quantise(diff, codes, scales):
+            nc.vector.quantize_mx(
+                out=codes.rearrange("p s n -> p (s n)").bitcast(FP8X4),
+                scales=scales.rearrange("p s n -> p (s n)"),
+                in_=diff.rearrange("p s n t -> p (s n t)"),
+            )
+
+        def multiply(out, codes, scales, s, tokens):
+            nc.tensor.matmul_mx(
+                out=out,
+                lhsT=codes[:, s, tokens].bitcast(FP8X4),
+                lhsT_scale=scales[:, s, tokens],
+                rhs=u_codes[:, s, :].bitcast(FP8X4),
+                rhs_scale=u_scales[:, s, :],
+                start=True,
+                stop=True,
+            )
+
+        def square(out, proj, s, j):
+            nc.scalar.activation(out=out, in_=proj, func=ACT.Square, accum_out=sumsq[:, s, j : j + 1])
 
         def project(diff, tiles):
             codes = mx_pool.tile([P, SOURCES, len(tiles) * P], U32, align_bytes=64)
             scales = mx_pool.tile([P, SOURCES, len(tiles) * P], U8, align_bytes=64)
-            nc.vector.quantize_mx(
-                out=codes[:].rearrange("p s n -> p (s n)").bitcast(FP8X4),
-                scales=scales[:].rearrange("p s n -> p (s n)"),
-                in_=diff[:].rearrange("p s n t -> p (s n t)"),
-            )
+            quantise(diff[:], codes[:], scales[:])
             for i, j in enumerate(tiles):
-                tokens = slice(i * P, (i + 1) * P)
                 proj = proj_psum.tile([P, SOURCES, RANK], F32)
-                for s in range(SOURCES):
-                    nc.tensor.matmul_mx(
-                        out=proj[:, s, :],
-                        lhsT=codes[:, s, tokens].bitcast(FP8X4),
-                        lhsT_scale=scales[:, s, tokens],
-                        rhs=u_codes[:, s, :].bitcast(FP8X4),
-                        rhs_scale=u_scales[:, s, :],
-                        start=True,
-                        stop=True,
-                    )
                 squares = square_pool.tile([P, SOURCES, RANK], F32)
                 for s in range(SOURCES):
-                    nc.scalar.activation(
-                        out=squares[:, s, :], in_=proj[:, s, :], func=ACT.Square, accum_out=sumsq[:, s, j : j + 1]
-                    )
+                    multiply(proj[:, s, :], codes, scales, s, slice(i * P, (i + 1) * P))
+                for s in range(SOURCES):
+                    square(squares[:, s, :], proj[:, s, :], s, j)
 
-        def project_by_source(diff, j):
+        def project_by_source(diff, j, calls):
             codes = mx_pool.tile([P, SOURCES, P], U32, align_bytes=64)
             scales = mx_pool.tile([P, SOURCES, P], U8, align_bytes=64)
             squares = square_pool.tile([P, SOURCES, RANK], F32)
+            each = SOURCES // calls
             for s in range(SOURCES):
-                nc.vector.quantize_mx(
-                    out=codes[:, s, :].bitcast(FP8X4),
-                    scales=scales[:, s, :],
-                    in_=diff[:, s, :, :].rearrange("p n t -> p (n t)"),
-                )
-                proj = proj_psum.tile([P, RANK], F32)
-                nc.tensor.matmul_mx(
-                    out=proj[:],
-                    lhsT=codes[:, s, :].bitcast(FP8X4),
-                    lhsT_scale=scales[:, s, :],
-                    rhs=u_codes[:, s, :].bitcast(FP8X4),
-                    rhs_scale=u_scales[:, s, :],
-                    start=True,
-                    stop=True,
-                )
-                nc.scalar.activation(
-                    out=squares[:, s, :], in_=proj[:], func=ACT.Square, accum_out=sumsq[:, s, j : j + 1]
-                )
+                if s % each == 0:
+                    part = slice(s, s + each)
+                    quantise(diff[:, part, :, :], codes[:, part, :], scales[:, part, :])
+                if s % 2 == 0:
+                    proj = proj_psum.tile([P, RANK], F32)
+                else:
+                    proj = made_psum.tile([P, RANK], F32, name="made")
+                multiply(proj[:], codes, scales, s, slice(0, P))
+                square(squares[:, s, :], proj[:], s, j)
 
         pieces = []
         for made_g in MADE_GROUPS:
@@ -285,35 +291,60 @@ def tile_moe_pa_e_kernel(tc, encodings, domain_encs, Us_words, Us_scales, out):
                 pieces.extend([(add_up, made_g, s) for s in range(SOURCES)])
             else:
                 pieces.extend([(make, made_g, c) for c in range(CHUNKS)])
-        piece_steps = MADE_GROUPS[-1] - 1 - FIRST_PIECE_STEP
-        for g in range(AHEAD):
-            turn(g)
-        subtract(0)
-        nc.scalar.activation(out=neg_t[:], in_=dom_t[:], func=ACT.Copy, scale=-1.0)
-        for s in range(SOURCES):
-            spread_dom(s)
-        for g in range(len(groups)):
-            if g + 1 < len(groups):
-                subtract(g + 1)
+        piece_steps = MADE_GROUPS[-1] - MADE_AHEAD + 1 - FIRST_PIECE_STEP
+
+        def prepare(g):
             if g + AHEAD < len(groups):
                 turn(g + AHEAD)
             for q, piece in enumerate(pieces):
                 if FIRST_PIECE_STEP + q * piece_steps // len(pieces) == g:
-                    assert g <= piece[1] - 2
+                    assert g <= piece[1] - MADE_AHEAD
                     piece[0](piece[1], piece[2])
-            if g == len(groups) - EDGE_SINGLES:
-                nc.scalar.activation(out=dist[:, :, : groups[g][0]], in_=sumsq[:, :, : groups[g][0]], func=ACT.Sqrt)
+
+        def project_made(g):
             if g in MADE_GROUPS:
                 project(made_diffs[g], groups[g][:1])
-                project(diffs[g], groups[g][1:])
-            elif g + 1 < len(groups):
-                project(diffs[g], groups[g])
-            else:
-                project_by_source(diffs[g], groups[g][0])
+
+        for g in range(AHEAD):
+            turn(g)
+        nc.scalar.activation(out=neg_t[:], in_=dom_t[:], func=ACT.Copy, scale=-1.0)
+        for s in range(SOURCES):
+            spread_dom(s)
+        for first in range(0, len(groups) - FINE_GROUPS, BATCH):
+            batch = range(first, first + BATCH)
+            for g in batch:
+                subtract(g)
+            for g in batch:
+                prepare(g)
+            for g in batch:
+                project_made(g)
+            for g in batch:
+                project(diffs[g], subtracted(g))
+        a, b, c, d, e, f = range(len(groups) - FINE_GROUPS, len(groups))
+        half = SOURCES // 2
+        subtract(a)
+        subtract(b)
+        prepare(a)
+        prepare(b)
+        project(diffs[a], subtracted(a))
+        project_made(b)
+        subtract(c)
+        prepare(c)
+        project_made(d)
+        project(diffs[b], subtracted(b))
+        project(diffs[c], subtracted(c))
+        early = slice(0, TILES - LATE_TILES)
+        nc.scalar.activation(out=dist[:, :, early], in_=sumsq[:, :, early], func=ACT.Sqrt)
+        subtract(d)
+        subtract(e)
+        project_by_source(diffs[d], subtracted(d)[0], 1)
+        project_by_source(diffs[e], subtracted(e)[0], 1)
+        subtract(f, (slice(0, half), slice(half, SOURCES)))
+        project_by_source(diffs[f], subtracted(f)[0], SOURCES)
 
         by_token = "p s j -> p j s"
         spread = [P, SOURCES, TILES]
-        late = slice(TILES - EDGE_SINGLES, TILES)
+        late = slice(TILES - LATE_TILES, TILES)
         nc.scalar.activation(out=dist[:, :, late], in_=sumsq[:, :, late], func=ACT.Sqrt)
         nearest = keep.tile([P, TILES], F32)
         nc.vector.tensor_reduce(out=nearest[:], in_=dist[:].rearrange(by_token), axis=AXIS.X, op=ALU.min)

@@ -36,10 +36,11 @@ PLAIN_GROUPS = (7, 11, 15)
 SUMMED_GROUPS = (9, 13)
 MADE_GROUPS = tuple(sorted(PLAIN_GROUPS + SUMMED_GROUPS))
 FIRST_PIECE_STEP = 2
-MADE_AHEAD = 4
-TOKEN_ROWS = P - SOURCES
-CHUNK = 32
-CHUNKS = P // CHUNK
+MADE_AHEAD = 3
+PAIR = 2
+TOKEN_ROWS = 32
+OPERANDS = P // TOKEN_ROWS
+OPERANDS_EACH = 2
 
 FLOPS = 2 * SOURCES * TOKENS * HIDDEN * RANK
 
@@ -102,37 +103,40 @@ def tile_moe_pa_e_kernel(tc, encodings, domain_encs, Us_words, Us_scales, out):
                 out=u_scales[row:P:QUADRANT, :, :].bitcast(I32), in_=scale_rows[row].bitcast(I32)
             )
 
-        sel = keep.tile([P, CHUNKS, SOURCES, CHUNK], BF16)
-        low_shape = [P, CHUNKS - 1, SOURCES, CHUNK]
+        sel = keep.tile([P, SOURCES, TOKEN_ROWS, PAIR], BF16)
+        sel_shape = [P, SOURCES, TOKEN_ROWS, PAIR]
+        first_source = PAIR * TOKEN_ROWS
+        source_rows = ident[:, first_source : first_source + PAIR * SOURCES]
         nc.gpsimd.tensor_tensor(
-            out=sel[:, : CHUNKS - 1, :, :],
-            in0=ident[:, : P - CHUNK].rearrange("p (c n) -> p c n", n=CHUNK).unsqueeze(2).to_broadcast(low_shape),
-            in1=ident[:, TOKEN_ROWS:].unsqueeze(1).unsqueeze(3).to_broadcast(low_shape),
+            out=sel[:],
+            in0=ident[:, :first_source].rearrange("p (u n) -> p n u", u=PAIR).unsqueeze(1).to_broadcast(sel_shape),
+            in1=source_rows.rearrange("p (u s) -> p s u", u=PAIR).unsqueeze(2).to_broadcast(sel_shape),
             op=ALU.subtract,
         )
-        high_shape = [P, SOURCES, CHUNK]
-        nc.gpsimd.tensor_tensor(
-            out=sel[:, CHUNKS - 1, :, :],
-            in0=ident[:, TOKEN_ROWS - CHUNK : TOKEN_ROWS].unsqueeze(1).to_broadcast(high_shape),
-            in1=ident[:, TOKEN_ROWS:].unsqueeze(2).to_broadcast(high_shape),
-            op=ALU.subtract,
-        )
-        augs = {}
+        augs = keep.tile([P, OPERANDS, HIDDEN], BF16)
+        nc.vector.memset(augs[first_source:, :, :].bitcast(I32), 0)
+
+        def load_sources():
+            for u in range(PAIR):
+                rows = slice(first_source + u * SOURCES, first_source + (u + 1) * SOURCES)
+                nc.sync.dma_start(
+                    out=augs[rows, :, : HIDDEN - u],
+                    in_=domain_encs[:, u:].unsqueeze(1).to_broadcast([SOURCES, OPERANDS, HIDDEN - u]),
+                )
 
         def subtracted(g):
             return groups[g][1:] if g in MADE_GROUPS else groups[g]
 
         def load_made(g):
-            low = keep.tile([P, HIDDEN], BF16, name="low%d" % g)
-            high = keep.tile([P, HIDDEN], BF16, name="high%d" % g)
-            nc.sync.dma_start(out=low[:TOKEN_ROWS, :], in_=enc_rows[:TOKEN_ROWS, groups[g][0], :])
-            nc.sync.dma_start(out=low[TOKEN_ROWS:, :], in_=domain_encs)
-            nc.sync.dma_start(out=high[:TOKEN_ROWS, :], in_=enc_rows[SOURCES:, groups[g][0], :])
-            nc.sync.dma_start(out=high[TOKEN_ROWS:, :], in_=domain_encs)
-            augs[g] = (low, high)
+            for u in range(PAIR):
+                nc.sync.dma_start(
+                    out=augs[u * TOKEN_ROWS : (u + 1) * TOKEN_ROWS, :, : HIDDEN - u],
+                    in_=enc_rows[:, groups[g][0], u:].rearrange("(c i) h -> i c h", c=OPERANDS),
+                )
 
         for g in range(len(groups)):
-            if g + 3 in PLAIN_GROUPS:
+            if g + 3 == PLAIN_GROUPS[0]:
+                load_sources()
                 load_made(g + 3)
             if g + 4 in SUMMED_GROUPS:
                 load_tokens(groups[g + 4][0])
@@ -167,23 +171,23 @@ def tile_moe_pa_e_kernel(tc, encodings, domain_encs, Us_words, Us_scales, out):
             nc.scalar.copy(out=side[:].bitcast(F32), in_=turned[:, tokens - gp_tokens(g) :, :])
             sides[g] = side
 
-        def make(g, c):
-            if c == 0:
+        def make(g, first):
+            if first == 0:
                 made_diffs[g] = made_pool.tile([P, SOURCES, P, PACK], BF16, align_bytes=64, name="made_diff")
-            made = made_psum.tile([P, PACK, SOURCES, CHUNK], F32)
-            aug = augs[g][1 if c == CHUNKS - 1 else 0]
-            for t in range(PACK):
-                nc.tensor.matmul(
-                    out=made[:, t, :, :].rearrange("p s n -> p (s n)"),
-                    lhsT=aug[:, t:HIDDEN:PACK],
-                    rhs=sel[:, c, :, :].rearrange("p s n -> p (s n)"),
-                    start=True,
-                    stop=True,
-                )
-            nc.scalar.copy(
-                out=made_diffs[g][:, :, c * CHUNK : (c + 1) * CHUNK, :],
-                in_=made[:].rearrange("p t s n -> p s n t"),
-            )
+            made = made_psum.tile([P, SOURCES, OPERANDS_EACH * TOKEN_ROWS, PACK], BF16)
+            for c in range(OPERANDS_EACH):
+                for t in range(0, PACK, PAIR):
+                    nc.tensor.matmul(
+                        out=made[:, :, c * TOKEN_ROWS : (c + 1) * TOKEN_ROWS, t : t + PAIR],
+                        lhsT=augs[:, first + c, t:HIDDEN:PACK],
+                        rhs=sel[:],
+                        start=True,
+                        stop=True,
+                    )
+            tokens = slice(first * TOKEN_ROWS, (first + OPERANDS_EACH) * TOKEN_ROWS)
+            nc.scalar.copy(out=made_diffs[g][:, :, tokens, :], in_=made[:])
+            if first + OPERANDS_EACH == OPERANDS and g != PLAIN_GROUPS[-1]:
+                load_made(PLAIN_GROUPS[PLAIN_GROUPS.index(g) + 1])
 
         neg_t = keep.tile([P, SOURCES, PACK], F32)
         neg_dom = keep.tile([P, SOURCES, PACK, P], F32)
@@ -290,7 +294,7 @@ def tile_moe_pa_e_kernel(tc, encodings, domain_encs, Us_words, Us_scales, out):
                 pieces.append((widen, made_g, 0))
                 pieces.extend([(add_up, made_g, s) for s in range(SOURCES)])
             else:
-                pieces.extend([(make, made_g, c) for c in range(CHUNKS)])
+                pieces.extend([(make, made_g, first) for first in range(0, OPERANDS, OPERANDS_EACH)])
         piece_steps = MADE_GROUPS[-1] - MADE_AHEAD + 1 - FIRST_PIECE_STEP
 
         def prepare(g):

from contextlib import ExitStack

import concourse.mybir as mybir
from concourse.masks import make_identity

F32 = mybir.dt.float32
BF16 = mybir.dt.bfloat16
I32 = mybir.dt.int32
U32 = mybir.dt.uint32
U8 = mybir.dt.uint8
FP8X4 = mybir.dt.float8_e4m3fn_x4
ACT = mybir.ActivationFunctionType
ALU = mybir.AluOpType
AXIS = mybir.AxisListType

P = 128
TOKENS = 4096
HIDDEN = 512
SOURCES = 4
RANK = 128
PACK = 4
HALVES = 2
QUADRANT = 32
LIVE_ROWS = 4
TILES = TOKENS // P
EDGE_SINGLES = 2
BATCH = 2
FINE_GROUPS = 6
LATE_TILES = 6
EARLY_TILES = 4
AHEAD = 3
PROJ_BANKS = 3
MADE_BANKS = 2
GP_TOKENS = (0, 20, 44)
PLAIN_GROUPS = (7, 11, 15)
SUMMED_GROUPS = (9, 13)
MADE_GROUPS = tuple(sorted(PLAIN_GROUPS + SUMMED_GROUPS))
FIRST_PIECE_STEP = 2
MADE_AHEAD = 3
PAIR = 2
TOKEN_ROWS = 32
OPERANDS = P // TOKEN_ROWS
OPERANDS_EACH = 2

FLOPS = 2 * SOURCES * TOKENS * HIDDEN * RANK


def token_groups():
    groups = [(j,) for j in range(EDGE_SINGLES)]
    groups.extend([(j, j + 1) for j in range(EDGE_SINGLES, TILES - EDGE_SINGLES, 2)])
    groups.extend([(j,) for j in range(TILES - EDGE_SINGLES, TILES)])
    return groups


def tile_moe_pa_e_kernel(tc, encodings, domain_encs, Us_words, Us_scales, out):
    nc = tc.nc
    groups = token_groups()
    with ExitStack() as ctx:
        ctx.enter_context(tc.manual_schedule(engines={mybir.EngineType.DVE, mybir.EngineType.Pool}))
        keep = ctx.enter_context(tc.tile_pool(name="keep", bufs=1))
        side_pool = ctx.enter_context(tc.tile_pool(name="side_pool", bufs=AHEAD))
        diff_pool = ctx.enter_context(tc.tile_pool(name="diff_pool", bufs=2))
        made_pool = ctx.enter_context(tc.tile_pool(name="made_pool", bufs=5))
        wide_pool = ctx.enter_context(tc.tile_pool(name="wide_pool", bufs=2))
        mx_pool = ctx.enter_context(tc.tile_pool(name="mx_pool", bufs=8))
        square_pool = ctx.enter_context(tc.tile_pool(name="square_pool", bufs=PROJ_BANKS))
        turned_psum = ctx.enter_context(tc.psum_pool(name="turned_psum", bufs=AHEAD))
        proj_psum = ctx.enter_context(tc.psum_pool(name="proj_psum", bufs=PROJ_BANKS))
        made_psum = ctx.enter_context(tc.psum_pool(name="made_psum", bufs=MADE_BANKS))

        enc_rows = encodings.rearrange("(p j) h -> p j h", j=TILES)
        enc_sb = keep.tile([P, TILES, HIDDEN], BF16)

        def load_tokens(j):
            nc.sync.dma_start(out=enc_sb[:, j, :], in_=enc_rows[:, j, :])

        load_tokens(0)

        dom_t = keep.tile([P, SOURCES, PACK], BF16)
        nc.scalar.dma_start(out=dom_t[:], in_=domain_encs.rearrange("s (p t) -> p s t", t=PACK))

        one = keep.tile([P, 1], F32)
        nc.vector.memset(one[:], 1.0)
        warm = keep.tile([P, 1], F32)
        nc.scalar.activation(out=warm[:], in_=one[:], func=ACT.Sqrt)

        ident = keep.tile([P, P], F32)
        make_identity(nc, ident[:])

        for j in range(1, EARLY_TILES):
            load_tokens(j)

        u_codes = keep.tile([P, SOURCES, RANK], U32, align_bytes=64)
        nc.sync.dma_start(
            out=u_codes[:].bitcast(I32),
            in_=Us_words.rearrange("s p r t -> p s (r t)").bitcast(I32),
        )
        u_scales = keep.tile([P, SOURCES, RANK], U8, align_bytes=64)
        nc.vector.memset(u_scales[:].bitcast(I32), 0)
        scale_rows = Us_scales.rearrange("s (quad row) r -> row quad s r", row=LIVE_ROWS)
        for row in range(LIVE_ROWS):
            nc.sync.dma_start(
                out=u_scales[row:P:QUADRANT, :, :].bitcast(I32), in_=scale_rows[row].bitcast(I32)
            )

        sel = keep.tile([P, SOURCES, TOKEN_ROWS, PAIR], BF16)
        sel_shape = [P, SOURCES, TOKEN_ROWS, PAIR]
        first_source = PAIR * TOKEN_ROWS
        source_rows = ident[:, first_source : first_source + PAIR * SOURCES]
        nc.gpsimd.tensor_tensor(
            out=sel[:],
            in0=ident[:, :first_source].rearrange("p (u n) -> p n u", u=PAIR).unsqueeze(1).to_broadcast(sel_shape),
            in1=source_rows.rearrange("p (u s) -> p s u", u=PAIR).unsqueeze(2).to_broadcast(sel_shape),
            op=ALU.subtract,
        )
        augs = keep.tile([P, OPERANDS, HIDDEN], BF16)
        nc.vector.memset(augs[first_source:, :, :].bitcast(I32), 0)

        def load_sources():
            for u in range(PAIR):
                rows = slice(first_source + u * SOURCES, first_source + (u + 1) * SOURCES)
                nc.sync.dma_start(
                    out=augs[rows, :, : HIDDEN - u],
                    in_=domain_encs[:, u:].unsqueeze(1).to_broadcast([SOURCES, OPERANDS, HIDDEN - u]),
                )

        def subtracted(g):
            return groups[g][1:] if g in MADE_GROUPS else groups[g]

        def load_made(g):
            for u in range(PAIR):
                nc.sync.dma_start(
                    out=augs[u * TOKEN_ROWS : (u + 1) * TOKEN_ROWS, :, : HIDDEN - u],
                    in_=enc_rows[:, groups[g][0], u:].rearrange("(c i) h -> i c h", c=OPERANDS),
                )

        for g in range(len(groups)):
            if g + 3 == PLAIN_GROUPS[0]:
                load_sources()
                load_made(g + 3)
            if g + 4 in SUMMED_GROUPS:
                load_tokens(groups[g + 4][0])
            for j in subtracted(g):
                if j >= EARLY_TILES:
                    load_tokens(j)

        sumsq = keep.tile([P, SOURCES, TILES], F32)
        dist = keep.tile([P, SOURCES, TILES], F32)
        turneds = {}
        sides = {}
        diffs = {}
        made_diffs = {}

        def gp_tokens(g):
            return GP_TOKENS[len(subtracted(g))]

        def turn(g):
            tiles = subtracted(g)
            tokens = len(tiles) * P
            turned = turned_psum.tile([P, tokens, HALVES], F32)
            for i, j in enumerate(tiles):
                words = enc_sb[:, j, :].bitcast(F32)
                for u in range(HALVES):
                    nc.tensor.transpose(
                        out=turned[:, i * P : (i + 1) * P, u],
                        in_=words[:, u : HIDDEN // 2 : HALVES],
                        identity=ident[:],
                    )
            turneds[g] = turned
            side = side_pool.tile([P, gp_tokens(g), PACK], BF16)
            nc.scalar.copy(out=side[:].bitcast(F32), in_=turned[:, tokens - gp_tokens(g) :, :])
            sides[g] = side

        def make(g, first):
            if first == 0:
                made_diffs[g] = made_pool.tile([P, SOURCES, P, PACK], BF16, align_bytes=64, name="made_diff")
            made = made_psum.tile([P, SOURCES, OPERANDS_EACH * TOKEN_ROWS, PACK], BF16)
            for c in range(OPERANDS_EACH):
                for t in range(0, PACK, PAIR):
                    nc.tensor.matmul(
                        out=made[:, :, c * TOKEN_ROWS : (c + 1) * TOKEN_ROWS, t : t + PAIR],
                        lhsT=augs[:, first + c, t:HIDDEN:PACK],
                        rhs=sel[:],
                        start=True,
                        stop=True,
                    )
            tokens = slice(first * TOKEN_ROWS, (first + OPERANDS_EACH) * TOKEN_ROWS)
            nc.scalar.copy(out=made_diffs[g][:, :, tokens, :], in_=made[:])
            if first + OPERANDS_EACH == OPERANDS and g != PLAIN_GROUPS[-1]:
                load_made(PLAIN_GROUPS[PLAIN_GROUPS.index(g) + 1])

        neg_t = keep.tile([P, SOURCES, PACK], F32)
        neg_dom = keep.tile([P, SOURCES, PACK, P], F32)
        wides = {}

        def spread_dom(s):
            made = made_psum.tile([P, PACK, P], F32)
            for t in range(PACK):
                nc.tensor.transpose(
                    out=made[:, t, :], in_=neg_t[:, s, t : t + 1].to_broadcast([P, P]), identity=ident[:]
                )
            nc.scalar.copy(out=neg_dom[:, s, :, :], in_=made[:])

        def widen(g, unused):
            made_diffs[g] = made_pool.tile([P, SOURCES, P, PACK], BF16, align_bytes=64, name="made_diff")
            wide = wide_pool.tile([P, PACK, P], F32)
            nc.scalar.copy(out=wide[:], in_=enc_sb[:, groups[g][0], :].rearrange("n (p t) -> n t p", t=PACK))
            wides[g] = wide

        def add_up(g, s):
            made = made_psum.tile([P, PACK, P], F32)
            for t in range(PACK):
                nc.tensor.matmul(
                    out=made[:, t, :], lhsT=neg_dom[:, s, t, :], rhs=ident[:], is_transpose=True, start=True, stop=False
                )
                nc.tensor.matmul(
                    out=made[:, t, :], lhsT=wides[g][:, t, :], rhs=ident[:], is_transpose=True, start=False, stop=True
                )
            nc.scalar.copy(out=made_diffs[g][:, s, :, :], in_=made[:].rearrange("p t n -> p n t"))

        every_source = slice(0, SOURCES)

        def minus(engine, diff, tokens, sources=every_source):
            shape = [P, sources.stop - sources.start, tokens.shape[1], PACK]
            engine.tensor_tensor(
                out=diff[:, sources, :, :],
                in0=tokens.unsqueeze(1).to_broadcast(shape),
                in1=dom_t[:, sources, :].unsqueeze(2).to_broadcast(shape),
                op=ALU.subtract,
            )

        def subtract(g, parts=(every_source,)):
            width = len(subtracted(g)) * P
            ve_tokens = width - gp_tokens(g)
            diff = diff_pool.tile([P, SOURCES, width, PACK], BF16, align_bytes=64)
            diffs[g] = diff
            as_bf16 = turneds[g][:].bitcast(BF16)
            minus(nc.gpsimd, diff[:, :, ve_tokens:, :], sides[g][:])
            for part in parts:
                minus(nc.vector, diff[:, :, :ve_tokens, :], as_bf16[:, :ve_tokens, :], part)

        def quantise(diff, codes, scales):
            nc.vector.quantize_mx(
                out=codes.rearrange("p s n -> p (s n)").bitcast(FP8X4),
                scales=scales.rearrange("p s n -> p (s n)"),
                in_=diff.rearrange("p s n t -> p (s n t)"),
            )

        def multiply(out, codes, scales, s, tokens):
            nc.tensor.matmul_mx(
                out=out,
                lhsT=codes[:, s, tokens].bitcast(FP8X4),
                lhsT_scale=scales[:, s, tokens],
                rhs=u_codes[:, s, :].bitcast(FP8X4),
                rhs_scale=u_scales[:, s, :],
                start=True,
                stop=True,
            )

        def square(out, proj, s, j):
            nc.scalar.activation(out=out, in_=proj, func=ACT.Square, accum_out=sumsq[:, s, j : j + 1])

        def project(diff, tiles):
            codes = mx_pool.tile([P, SOURCES, len(tiles) * P], U32, align_bytes=64)
            scales = mx_pool.tile([P, SOURCES, len(tiles) * P], U8, align_bytes=64)
            quantise(diff[:], codes[:], scales[:])
            for i, j in enumerate(tiles):
                proj = proj_psum.tile([P, SOURCES, RANK], F32)
                squares = square_pool.tile([P, SOURCES, RANK], F32)
                for s in range(SOURCES):
                    multiply(proj[:, s, :], codes, scales, s, slice(i * P, (i + 1) * P))
                for s in range(SOURCES):
                    square(squares[:, s, :], proj[:, s, :], s, j)

        def project_by_source(diff, j, calls):
            codes = mx_pool.tile([P, SOURCES, P], U32, align_bytes=64)
            scales = mx_pool.tile([P, SOURCES, P], U8, align_bytes=64)
            squares = square_pool.tile([P, SOURCES, RANK], F32)
            each = SOURCES // calls
            for s in range(SOURCES):
                if s % each == 0:
                    part = slice(s, s + each)
                    quantise(diff[:, part, :, :], codes[:, part, :], scales[:, part, :])
                if s % 2 == 0:
                    proj = proj_psum.tile([P, RANK], F32)
                else:
                    proj = made_psum.tile([P, RANK], F32, name="made")
                multiply(proj[:], codes, scales, s, slice(0, P))
                square(squares[:, s, :], proj[:], s, j)

        pieces = []
        for made_g in MADE_GROUPS:
            if made_g in SUMMED_GROUPS:
                pieces.append((widen, made_g, 0))
                pieces.extend([(add_up, made_g, s) for s in range(SOURCES)])
            else:
                pieces.extend([(make, made_g, first) for first in range(0, OPERANDS, OPERANDS_EACH)])
        piece_steps = MADE_GROUPS[-1] - MADE_AHEAD + 1 - FIRST_PIECE_STEP

        def prepare(g):
            if g + AHEAD < len(groups):
                turn(g + AHEAD)
            for q, piece in enumerate(pieces):
                if FIRST_PIECE_STEP + q * piece_steps // len(pieces) == g:
                    assert g <= piece[1] - MADE_AHEAD
                    piece[0](piece[1], piece[2])

        def project_made(g):
            if g in MADE_GROUPS:
                project(made_diffs[g], groups[g][:1])

        for g in range(AHEAD):
            turn(g)
        nc.scalar.activation(out=neg_t[:], in_=dom_t[:], func=ACT.Copy, scale=-1.0)
        for s in range(SOURCES):
            spread_dom(s)
        for first in range(0, len(groups) - FINE_GROUPS, BATCH):
            batch = range(first, first + BATCH)
            for g in batch:
                subtract(g)
            for g in batch:
                prepare(g)
            for g in batch:
                project_made(g)
            for g in batch:
                project(diffs[g], subtracted(g))
        a, b, c, d, e, f = range(len(groups) - FINE_GROUPS, len(groups))
        half = SOURCES // 2
        subtract(a)
        subtract(b)
        prepare(a)
        prepare(b)
        project(diffs[a], subtracted(a))
        project_made(b)
        subtract(c)
        prepare(c)
        project_made(d)
        project(diffs[b], subtracted(b))
        project(diffs[c], subtracted(c))
        early = slice(0, TILES - LATE_TILES)
        nc.scalar.activation(out=dist[:, :, early], in_=sumsq[:, :, early], func=ACT.Sqrt)
        subtract(d)
        subtract(e)
        project_by_source(diffs[d], subtracted(d)[0], 1)
        project_by_source(diffs[e], subtracted(e)[0], 1)
        subtract(f, (slice(0, half), slice(half, SOURCES)))
        project_by_source(diffs[f], subtracted(f)[0], SOURCES)

        by_token = "p s j -> p j s"
        spread = [P, SOURCES, TILES]
        late = slice(TILES - LATE_TILES, TILES)
        nc.scalar.activation(out=dist[:, :, late], in_=sumsq[:, :, late], func=ACT.Sqrt)
        nearest = keep.tile([P, TILES], F32)
        nc.vector.tensor_reduce(out=nearest[:], in_=dist[:].rearrange(by_token), axis=AXIS.X, op=ALU.min)
        excess = keep.tile(spread, F32)
        nc.vector.tensor_tensor(
            out=excess[:], in0=dist[:], in1=nearest[:].unsqueeze(1).to_broadcast(spread), op=ALU.subtract
        )
        weight = keep.tile(spread, F32)
        nc.scalar.activation(out=weight[:], in_=excess[:], func=ACT.Exp, scale=-1.0)
        total = keep.tile([P, TILES], F32)
        inverse = keep.tile([P, TILES], F32)
        alphas = keep.tile(spread, F32)
        halves = (slice(0, TILES // 2), slice(TILES // 2, TILES))
        half_spread = [P, SOURCES, TILES // 2]
        for half in halves:
            nc.vector.tensor_reduce(
                out=total[:, half], in_=weight[:, :, half].rearrange(by_token), axis=AXIS.X, op=ALU.add
            )
        for half in halves:
            nc.vector.reciprocal(out=inverse[:, half], in_=total[:, half])
        out_by_tile = out.rearrange("s (p j) -> p s j", j=TILES)
        for half, queue in zip(halves, (nc.sync, nc.scalar)):
            nc.vector.tensor_tensor(
                out=alphas[:, :, half],
                in0=weight[:, :, half],
                in1=inverse[:, half].unsqueeze(1).to_broadcast(half_spread),
                op=ALU.mult,
            )
            queue.dma_start(out=out_by_tile[:, :, half], in_=alphas[:, :, half])
